import numpy as np
import ml_dtypes


def mxq(x, axis, fmt="e4m3"):
    dtype, down = {"e4m3": (ml_dtypes.float8_e4m3fn, 7), "e5m2": (ml_dtypes.float8_e5m2, 14)}[fmt]
    v = np.moveaxis(np.asarray(x, np.float32).astype(ml_dtypes.bfloat16).astype(np.float64), axis, -1)
    blocks = v.reshape(v.shape[:-1] + (-1, 32))
    amax = np.abs(blocks).max(-1, keepdims=True)
    byte = np.maximum(np.where(amax > 0, np.frexp(amax)[1] - 1 + 127, 0) - down, 1)
    scale = np.exp2(byte - 127.0)
    codes = (blocks / scale).astype(np.float32).astype(dtype).astype(np.float64)
    return np.moveaxis((codes * scale).reshape(v.shape), -1, axis)


WIDE = False


def mx_kscale(k):
    if not WIDE:
        return np.ones(k)
    levels = np.array([10, -10, 5, -5, 0])
    if k % 512:
        return np.exp2(np.random.permutation(np.resize(levels, k // 32))).repeat(32)
    a = np.empty((k // 512, 16))
    for p in range(k // 512):
        a[p, :8] = np.random.permutation(np.resize(levels, 8))
        for g in range(8):
            far = levels[np.abs(levels - a[p, g]) >= 10]
            a[p, g + 8] = far[np.random.randint(len(far))]
    return np.exp2(a.ravel()).repeat(32)


BF16 = ml_dtypes.bfloat16


def bf(x):
    return np.asarray(x, np.float32).astype(BF16)


def f64(x):
    return np.asarray(x).astype(np.float64)


B, N, NIN, CTX, H, NOUT = 8, 512, 512, 3, 512, 2
F = NIN * CTX


def shift_down(y, d):
    return np.pad(y[:, :-d, :], ((0, 0), (d, 0), (0, 0)))


def shift_up(y, d):
    return np.pad(y[:, d:, :], ((0, 0), (0, d), (0, 0)))


def context_linear(xq, w, shifts):
    y = xq @ mxq(w[:, :NIN].T, 0, "e4m3")
    c = 1
    for d in range(1, CTX // 2 + 1):
        for shift in shifts:
            y = y + shift(xq @ mxq(w[:, c * NIN:(c + 1) * NIN].T, 0, "e4m3"), d)
            c += 1
    return y


def setup_inputs():
    s, u = mx_kscale(NIN), mx_kscale(H)
    return {"t_bil": bf(np.random.standard_normal((B, N, NOUT, H)) * 0.15 / u),
            "x_r": bf(np.random.standard_normal((B, N, NIN)) * s),
            "W_r": bf(np.random.standard_normal((H, F)) / np.sqrt(F) / np.tile(s, CTX) * u[:, None]),
            "b_r": bf(np.random.standard_normal(H) * 0.3 * u),
            "b_bil": bf(np.random.standard_normal(NOUT))}


def reference(t_bil, x_r, W_r, b_r, b_bil):
    xq = mxq(f64(x_r), 2, "e4m3")
    hr = np.maximum(context_linear(xq, f64(W_r), (shift_up, shift_down)) + f64(b_r), 0.0)
    tq = mxq(f64(t_bil).reshape(B, N * NOUT, H), 2, "e4m3")
    sc = tq @ mxq(hr.transpose(0, 2, 1), 1, "e4m3")
    return sc.reshape(B, N, NOUT, N).transpose(0, 1, 3, 2) + f64(b_bil)

@@ -1,0 +1,241 @@
+from contextlib import ExitStack
+
+import concourse.masks as masks
+import concourse.mybir as mybir
+
+F32 = mybir.dt.float32
+BF16 = mybir.dt.bfloat16
+U32 = mybir.dt.uint32
+U8 = mybir.dt.uint8
+FP8X4 = mybir.dt.float8_e4m3fn_x4
+ACT = mybir.ActivationFunctionType
+ALU = mybir.AluOpType
+
+P = 128
+B = 8
+FLOPS = 2 * 8 * 512 * 512 * 1536 + 2 * 8 * 1024 * 512 * 512
+
+MANUAL = True
+LAG = 6
+PLAN = (2, 2, 2, 0)
+AHEAD = 0
+RG = ("g", "g", "g", "s")
+HALO = "v"
+QDELAY = 1
+QHQ = 0
+NT = 6
+
+
+def tile_bilinearpairedlayer_pb_t_kernel(tc, t_bil, x_r, W_r, b_r, b_bil, out):
+    nc = tc.nc
+    with ExitStack() as ctx:
+        sb = ctx.enter_context(tc.tile_pool(name="sb", bufs=1))
+        ps = ctx.enter_context(tc.psum_pool(name="ps", bufs=1))
+
+        ident = sb.tile([P, P], F32, name="ident")
+        x_sb = [sb.tile([P, 2048], BF16, name="x%d" % i) for i in range(B)]
+        t_sb = [sb.tile([P, 4096], BF16, name="t%d" % i) for i in range(NT)]
+        w_sb = sb.tile([P, 6144], BF16, name="w_sb")
+        wg = sb.tile([P, 6144], BF16, name="wg", align_bytes=64)
+        wc = sb.tile([P, 1536], U32, name="wc", align_bytes=64)
+        ws = sb.tile([P, 1536], U8, name="ws", align_bytes=64)
+        xg = [sb.tile([P, 3072], BF16, name="xg%d" % i, align_bytes=64) for i in range(2)]
+        xc = [sb.tile([P, 768], U32, name="xc%d" % i, align_bytes=64) for i in range(3)]
+        xs = [sb.tile([P, 768], U8, name="xs%d" % i, align_bytes=64) for i in range(3)]
+        tg = [sb.tile([P, 2048], BF16, name="tg%d" % i, align_bytes=64) for i in range(4)]
+        tcd = [sb.tile([P, 1024], U32, name="tcd%d" % i, align_bytes=64) for i in range(3)]
+        tsc = [sb.tile([P, 1024], U8, name="tsc%d" % i, align_bytes=64) for i in range(3)]
+        hrt = [sb.tile([P, 2048], BF16, name="hrt%d" % i) for i in range(2)]
+        hg = [sb.tile([P, 2048], BF16, name="hg%d" % i, align_bytes=64) for i in range(2)]
+        hc = [sb.tile([P, 512], U32, name="hc%d" % i, align_bytes=64) for i in range(3)]
+        hs = [sb.tile([P, 512], U8, name="hs%d" % i, align_bytes=64) for i in range(3)]
+        o_sb = [sb.tile([P, 2048], F32, name="o%d" % i) for i in range(4)]
+        br_bf = sb.tile([P, 4], BF16, name="br_bf")
+        br = sb.tile([P, 4], F32, name="br")
+        bb_bf = sb.tile([P, 2], BF16, name="bb_bf")
+        bbt = sb.tile([P, 512], F32, name="bbt")
+        bbf = sb.tile([P, 2], F32, name="bbf")
+
+        pt = [ps.tile([P, 512], F32, name="pt%d" % i) for i in range(3)]
+        p1 = [ps.tile([P, 512], F32, name="p1_%d" % i) for i in range(2)]
+        p2 = [ps.tile([P, 512], F32, name="p2_%d" % i) for i in range(3)]
+        cnt = {"pt": 0, "p1": 0, "p2": 0, "o": 0}
+
+        if MANUAL:
+            ctx.enter_context(tc.manual_schedule())
+
+        def load_x(b):
+            nc.sync.dma_start(out=x_sb[b][:], in_=x_r[b].rearrange("(p a) f -> p (a f)", a=4))
+
+        def load_t(b):
+            nc.sync.dma_start(out=t_sb[b % NT][:], in_=t_bil[b].rearrange("(p a) k g -> p (a k g)", a=4))
+
+        w_view = W_r.rearrange("(p u e) f -> p u (e f)", u=2, e=2)
+        load_x(0)
+        for u in range(2):
+            nc.sync.dma_start(out=w_sb[:, u * 3072:(u + 1) * 3072], in_=w_view[:, u, :])
+        with nc.allow_non_contiguous_dma(reason="two small bias vectors"):
+            nc.scalar.dma_start(out=br_bf[:], in_=b_r.rearrange("(p t) -> p t", t=4))
+            nc.scalar.dma_start(out=bb_bf[:], in_=b_bil.partition_broadcast(P))
+        load_x(1)
+        for b in range(B):
+            if b + 2 < B:
+                load_x(b + 2)
+            if b < NT:
+                load_t(b)
+
+        masks.make_identity(nc, ident[:])
+        for i in range(2):
+            nc.vector.memset(xg[i][:, 0:4], 0.0)
+            nc.vector.memset(xg[i][:, 3068:3072], 0.0)
+        nc.vector.tensor_copy(out=br[:], in_=br_bf[:])
+        nc.vector.tensor_copy(out=bbf[:], in_=bb_bf[:])
+        nc.vector.tensor_copy(out=bbt[:].rearrange("p (j k) -> p j k", k=2),
+                              in_=bb_bf[:].unsqueeze(1).to_broadcast([P, 256, 2]))
+
+        def flip(src, m, dst, dst_off, eng):
+            bank = pt[cnt["pt"] % 3]
+            cnt["pt"] += 1
+            s32 = src[:].bitcast(F32)
+            for i in range(4):
+                c0 = 512 * m + 256 * (i // 2)
+                nc.tensor.transpose(bank[:, 128 * i:128 * (i + 1)], s32[:, c0 + i % 2:c0 + 256:2], ident[:])
+            o_ap = dst[:].bitcast(F32)[:, dst_off:dst_off + 512].rearrange("p (a c u) -> p a c u", a=2, u=2)
+            i_ap = bank[:].rearrange("p (a u c) -> p a c u", a=2, u=2)
+            if eng == "s":
+                nc.scalar.copy(out=o_ap, in_=i_ap)
+            else:
+                nc.vector.tensor_copy(out=o_ap, in_=i_ap)
+
+        def quant(codes, scales, c_off, src, s_off, width):
+            nc.vector.quantize_mx(out=codes[:, c_off:c_off + width // 4].bitcast(FP8X4),
+                                  scales=scales[:, c_off:c_off + width // 4],
+                                  in_=src[:, s_off:s_off + width])
+
+        def copy_on(eng, o_ap, i_ap):
+            if eng == "v":
+                nc.vector.tensor_copy(out=o_ap, in_=i_ap)
+            elif eng == "s":
+                nc.scalar.copy(out=o_ap, in_=i_ap)
+            else:
+                nc.gpsimd.tensor_scalar(out=o_ap, in0=i_ap, scalar1=1.0, scalar2=0.0, op0=ALU.mult, op1=ALU.add)
+
+        def job(kind, b, m, eng):
+            if kind == "x":
+                flip(x_sb[b], m, xg[b % 2], 256 + 512 * m, eng)
+                return [("x", b, 0)] if m == 1 else []
+            if kind == "w":
+                flip(w_sb, m, wg, 512 * m, eng)
+                return [("w", 0, m // 2)] if m % 2 == 1 else []
+            flip(t_sb[b % NT], m, tg[(2 * b + m // 2) % 4], 512 * (m % 2), eng)
+            if m == 3 and b + NT < B:
+                load_t(b + NT)
+            return [("t", b, m // 2)] if m % 2 == 1 else []
+
+        def quantise(kind, b, h):
+            if kind == "x":
+                g = xg[b % 2]
+                copy_on(HALO, g[:, 2560:3068], g[:, 516:1024])
+                copy_on(HALO, g[:, 4:512], g[:, 2048:2556])
+                quant(xc[b % 3], xs[b % 3], 0, g, 0, 2048)
+                quant(xc[b % 3], xs[b % 3], 512, g, 2048, 1024)
+            elif kind == "w":
+                quant(wc, ws, 512 * h, wg, 2048 * h, 2048)
+            else:
+                quant(tcd[b % 3], tsc[b % 3], 512 * h, tg[(2 * b + h) % 4], 0, 2048)
+
+        def s1(b, t):
+            bank = p1[cnt["p1"] % 2]
+            cnt["p1"] += 1
+            for w, off in ((0, 128), (1, 256), (2, 0)):
+                s = t * 3 + w
+                nc.tensor.matmul_mx(out=bank[:],
+                                    lhsT=wc[:, s * 128:(s + 1) * 128].bitcast(FP8X4),
+                                    lhsT_scale=ws[:, s * 128:(s + 1) * 128],
+                                    rhs=xc[b % 3][:, off:off + 512].bitcast(FP8X4),
+                                    rhs_scale=xs[b % 3][:, off:off + 512],
+                                    start=(w == 0), stop=(w == 2))
+            nc.scalar.activation(out=hrt[b % 2][:, t * 512:(t + 1) * 512].rearrange("p (q a) -> p q a", a=4),
+                                 in_=bank[:].rearrange("p (a q) -> p q a", a=4),
+                                 func=ACT.Relu, bias=br[:, t:t + 1], scale=1.0)
+
+        def regroup(b):
+            n = len(RG)
+            dst = hg[b % 2][:].rearrange("p (c i t) -> p c t i", i=4, t=4)
+            src = hrt[b % 2][:].rearrange("p (t c i) -> p c t i", t=4, i=4)
+            for i in range(n):
+                c0 = 128 * i // n
+                c1 = 128 * (i + 1) // n
+                copy_on(RG[i], dst[:, c0:c1], src[:, c0:c1])
+
+        def qh(b):
+            quant(hc[b % 3], hs[b % 3], 0, hg[b % 2], 0, 2048)
+
+        def s2(b, a):
+            if a % 2 == 0:
+                cnt["o"] += 1
+            o = o_sb[(cnt["o"] - 1) % 4]
+            for jh in range(2):
+                bank = p2[cnt["p2"] % 3]
+                cnt["p2"] += 1
+                for k in range(2):
+                    s = 2 * a + k
+                    nc.tensor.matmul_mx(out=bank[:, k * 256:(k + 1) * 256],
+                                        lhsT=tcd[b % 3][:, s * 128:(s + 1) * 128].bitcast(FP8X4),
+                                        lhsT_scale=tsc[b % 3][:, s * 128:(s + 1) * 128],
+                                        rhs=hc[b % 3][:, jh * 256:(jh + 1) * 256].bitcast(FP8X4),
+                                        rhs_scale=hs[b % 3][:, jh * 256:(jh + 1) * 256],
+                                        start=True, stop=True)
+                c0 = (a % 2) * 1024 + jh * 512
+                if a == 3 and jh == 1:
+                    for k in range(2):
+                        nc.scalar.activation(out=o[:, c0:c0 + 512].rearrange("p (j k) -> p j k", k=2)[:, :, k],
+                                             in_=bank[:, k * 256:(k + 1) * 256],
+                                             func=ACT.Identity, bias=bbf[:, k:k + 1], scale=1.0)
+                else:
+                    nc.vector.tensor_tensor(out=o[:, c0:c0 + 512].rearrange("p (j k) -> p j k", k=2),
+                                            in0=bank[:].rearrange("p (k j) -> p j k", k=2),
+                                            in1=bbt[:].rearrange("p (j k) -> p j k", k=2),
+                                            op=ALU.add)
+            o_view = out[b].rearrange("(p a) j k -> p a (j k)", a=4)
+            if b == B - 1:
+                nc.sync.dma_start(out=o_view[:, a, :], in_=o[:, (a % 2) * 1024:(a % 2 + 1) * 1024])
+            elif a % 2 == 1:
+                nc.sync.dma_start(out=o_view[:, a - 1:a + 1, :], in_=o[:].rearrange("p (a r) -> p a r", a=2))
+
+        jobs = [("x", 0, 0), ("x", 0, 1)] + [("w", 0, m) for m in range(6)] + [("x", 1, 0), ("x", 1, 1)]
+        for b in range(B):
+            if b + 2 < B:
+                jobs += [("x", b + 2, 0), ("x", b + 2, 1)]
+            jobs += [("t", b, m) for m in range(4)]
+        todo = []
+        for i in range(8 + AHEAD):
+            ready = todo
+            kind, b, m = jobs[i]
+            todo = job(kind, b, m, "v" if i % 2 else "s")
+            for kind, b, h in ready:
+                quantise(kind, b, h)
+        for kind, b, h in todo:
+            quantise(kind, b, h)
+        nxt = 8 + AHEAD
+        waiting = []
+        for tick in range(4 * B + LAG):
+            n = tick // 4
+            q = tick % 4
+            if q == 0 and 1 <= n <= B:
+                regroup(n - 1)
+            for i in range(PLAN[q]):
+                if nxt < len(jobs):
+                    kind, b, m = jobs[nxt]
+                    nxt += 1
+                    waiting += [(tick + QDELAY, item) for item in job(kind, b, m, "s")]
+            if n < B:
+                s1(n, q)
+            if tick >= LAG:
+                s2((tick - LAG) // 4, (tick - LAG) % 4)
+            if q == QHQ and 1 <= n <= B:
+                qh(n - 1)
+            for due, item in waiting:
+                if due <= tick:
+                    quantise(item[0], item[1], item[2])
+            waiting = [(due, item) for due, item in waiting if due > tick]

@@ -161,11 +161,11 @@ def tile_bilinearpairedlayer_pb_t_kernel(tc, t_bil, x_r, W_r, b_r, b_bil, out):
 
         def regroup(b):
             n = len(RG)
-            dst = hg[b % 2][:].rearrange("p (c i t) -> p c t i", i=4, t=4)
-            src = hrt[b % 2][:].rearrange("p (t c i) -> p c t i", t=4, i=4)
+            dst = hg[b % 2][:].rearrange("p (c t) -> p c t", t=4)
+            src = hrt[b % 2][:].rearrange("p (t c) -> p c t", t=4)
             for i in range(n):
-                c0 = 128 * i // n
-                c1 = 128 * (i + 1) // n
+                c0 = 512 * i // n
+                c1 = 512 * (i + 1) // n
                 copy_on(RG[i], dst[:, c0:c1], src[:, c0:c1])
 
         def qh(b):

@@ -13,17 +13,20 @@ ALU = mybir.AluOpType
 
 P = 128
 B = 8
+LAST = B - 1
 FLOPS = 2 * 8 * 512 * 512 * 1536 + 2 * 8 * 1024 * 512 * 512
 
-MANUAL = True
-LAG = 6
-PLAN = (2, 2, 2, 0)
-AHEAD = 0
-RG = ("g", "g", "g", "s")
-HALO = "v"
-QDELAY = 1
-QHQ = 0
-NT = 6
+BANKS_T, BANKS_1, BANKS_2 = 2, 2, 4
+HEAD = "vsvsssss"
+BTICK = 2
+PERM_M = ()
+QD = {"x": 1, "t": 1, "w": 0}
+SLOTS = ((0, 2, 2, 2), (2, 2, 0, 2))
+RG = ("v", "s")
+RG_END = ("v", "s")
+ON_S = ((7, 1, 0), (7, 3, 0), (7, 1, 1))
+NT = 4
+EXTRA = ()
 
 
 def tile_bilinearpairedlayer_pb_t_kernel(tc, t_bil, x_r, W_r, b_r, b_bil, out):
@@ -42,6 +45,10 @@ def tile_bilinearpairedlayer_pb_t_kernel(tc, t_bil, x_r, W_r, b_r, b_bil, out):
         xg = [sb.tile([P, 3072], BF16, name="xg%d" % i, align_bytes=64) for i in range(2)]
         xc = [sb.tile([P, 768], U32, name="xc%d" % i, align_bytes=64) for i in range(3)]
         xs = [sb.tile([P, 768], U8, name="xs%d" % i, align_bytes=64) for i in range(3)]
+        xg_end = sb.tile([P, 4096], BF16, name="xg_end", align_bytes=64)
+        xc_end = sb.tile([P, 1024], U32, name="xc_end", align_bytes=64)
+        xs_end = sb.tile([P, 1024], U8, name="xs_end", align_bytes=64)
+        tp = [sb.tile([P, 512], F32, name="tp%d" % i) for i in range(6)]
         tg = [sb.tile([P, 2048], BF16, name="tg%d" % i, align_bytes=64) for i in range(4)]
         tcd = [sb.tile([P, 1024], U32, name="tcd%d" % i, align_bytes=64) for i in range(3)]
         tsc = [sb.tile([P, 1024], U8, name="tsc%d" % i, align_bytes=64) for i in range(3)]
@@ -51,36 +58,45 @@ def tile_bilinearpairedlayer_pb_t_kernel(tc, t_bil, x_r, W_r, b_r, b_bil, out):
         hs = [sb.tile([P, 512], U8, name="hs%d" % i, align_bytes=64) for i in range(3)]
         o_sb = [sb.tile([P, 2048], F32, name="o%d" % i) for i in range(4)]
         br_bf = sb.tile([P, 4], BF16, name="br_bf")
+        rows = sb.tile([P, 2], BF16, name="rows")
+        ones = sb.tile([P, P], BF16, name="ones")
         br = sb.tile([P, 4], F32, name="br")
-        bb_bf = sb.tile([P, 2], BF16, name="bb_bf")
         bbt = sb.tile([P, 512], F32, name="bbt")
         bbf = sb.tile([P, 2], F32, name="bbf")
 
-        pt = [ps.tile([P, 512], F32, name="pt%d" % i) for i in range(3)]
-        p1 = [ps.tile([P, 512], F32, name="p1_%d" % i) for i in range(2)]
-        p2 = [ps.tile([P, 512], F32, name="p2_%d" % i) for i in range(3)]
-        cnt = {"pt": 0, "p1": 0, "p2": 0, "o": 0}
+        pt = [ps.tile([P, 512], F32, name="pt%d" % i) for i in range(BANKS_T)]
+        p1 = [ps.tile([P, 512], F32, name="p1_%d" % i) for i in range(BANKS_1)]
+        p2 = [ps.tile([P, 512], F32, name="p2_%d" % i) for i in range(BANKS_2)]
+        cnt = {"pt": 0, "p1": 0, "p2": 0}
 
-        if MANUAL:
-            ctx.enter_context(tc.manual_schedule())
+        ctx.enter_context(tc.manual_schedule())
 
         def load_x(b):
-            nc.sync.dma_start(out=x_sb[b][:], in_=x_r[b].rearrange("(p a) f -> p (a f)", a=4))
+            if b < LAST:
+                nc.sync.dma_start(out=x_sb[b][:], in_=x_r[b].rearrange("(p a) f -> p (a f)", a=4))
+            else:
+                nc.sync.dma_start(out=x_sb[b][:].rearrange("p (h r) -> p h r", h=2),
+                                  in_=x_r[b].rearrange("(h p a) f -> p h (a f)", h=2, a=2))
 
         def load_t(b):
             nc.sync.dma_start(out=t_sb[b % NT][:], in_=t_bil[b].rearrange("(p a) k g -> p (a k g)", a=4))
 
-        w_view = W_r.rearrange("(p u e) f -> p u (e f)", u=2, e=2)
-        load_x(0)
-        for u in range(2):
-            nc.sync.dma_start(out=w_sb[:, u * 3072:(u + 1) * 3072], in_=w_view[:, u, :])
-        with nc.allow_non_contiguous_dma(reason="two small bias vectors"):
+        x0_view = x_r[0].rearrange("(p a) f -> p (a f)", a=4)
+        for h in range(2):
+            nc.sync.dma_start(out=x_sb[0][:, 1024 * h:1024 * (h + 1)], in_=x0_view[:, 1024 * h:1024 * (h + 1)])
+        w_view = W_r.rearrange("(p t) f -> p (t f)", t=4)
+        for m in range(6):
+            nc.sync.dma_start(out=w_sb[:, 1024 * m:1024 * (m + 1)], in_=w_view[:, 1024 * m:1024 * (m + 1)])
+        with nc.allow_non_contiguous_dma(reason="four bfloat16 of b_r to a partition"):
             nc.scalar.dma_start(out=br_bf[:], in_=b_r.rearrange("(p t) -> p t", t=4))
-            nc.scalar.dma_start(out=bb_bf[:], in_=b_bil.partition_broadcast(P))
+        nc.vector.memset(rows[:], 0.0)
+        nc.vector.memset(ones[:], 1.0)
+        nc.scalar.dma_start(out=rows[0:1, :], in_=b_bil.unsqueeze(0))
+        load_t(0)
         load_x(1)
-        for b in range(B):
-            if b + 2 < B:
-                load_x(b + 2)
+        for b in range(1, B):
+            if b + 1 < B:
+                load_x(b + 1)
             if b < NT:
                 load_t(b)
 
@@ -88,55 +104,77 @@ def tile_bilinearpairedlayer_pb_t_kernel(tc, t_bil, x_r, W_r, b_r, b_bil, out):
         for i in range(2):
             nc.vector.memset(xg[i][:, 0:4], 0.0)
             nc.vector.memset(xg[i][:, 3068:3072], 0.0)
-        nc.vector.tensor_copy(out=br[:], in_=br_bf[:])
-        nc.vector.tensor_copy(out=bbf[:], in_=bb_bf[:])
-        nc.vector.tensor_copy(out=bbt[:].rearrange("p (j k) -> p j k", k=2),
-                              in_=bb_bf[:].unsqueeze(1).to_broadcast([P, 256, 2]))
+        nc.vector.memset(xg_end[:, 0:4], 0.0)
+        nc.vector.memset(xg_end[:, 4092:4096], 0.0)
 
-        def flip(src, m, dst, dst_off, eng):
-            bank = pt[cnt["pt"] % 3]
-            cnt["pt"] += 1
-            s32 = src[:].bitcast(F32)
-            for i in range(4):
-                c0 = 512 * m + 256 * (i // 2)
-                nc.tensor.transpose(bank[:, 128 * i:128 * (i + 1)], s32[:, c0 + i % 2:c0 + 256:2], ident[:])
-            o_ap = dst[:].bitcast(F32)[:, dst_off:dst_off + 512].rearrange("p (a c u) -> p a c u", a=2, u=2)
-            i_ap = bank[:].rearrange("p (a u c) -> p a c u", a=2, u=2)
-            if eng == "s":
-                nc.scalar.copy(out=o_ap, in_=i_ap)
-            else:
+        def next_bank(which, banks):
+            bank = banks[cnt[which] % len(banks)]
+            cnt[which] += 1
+            return bank
+
+        def copy_on(eng, o_ap, i_ap):
+            if eng == "v":
                 nc.vector.tensor_copy(out=o_ap, in_=i_ap)
+            else:
+                nc.scalar.copy(out=o_ap, in_=i_ap)
 
         def quant(codes, scales, c_off, src, s_off, width):
             nc.vector.quantize_mx(out=codes[:, c_off:c_off + width // 4].bitcast(FP8X4),
                                   scales=scales[:, c_off:c_off + width // 4],
                                   in_=src[:, s_off:s_off + width])
 
-        def copy_on(eng, o_ap, i_ap):
-            if eng == "v":
-                nc.vector.tensor_copy(out=o_ap, in_=i_ap)
-            elif eng == "s":
-                nc.scalar.copy(out=o_ap, in_=i_ap)
-            else:
-                nc.gpsimd.tensor_scalar(out=o_ap, in0=i_ap, scalar1=1.0, scalar2=0.0, op0=ALU.mult, op1=ALU.add)
+        def permute(b, m):
+            if m in PERM_M:
+                nc.scalar.copy(out=tp[(4 * b + m) % 6][:].rearrange("p (r u w) -> p r u w", r=2, u=2),
+                               in_=t_sb[b % NT][:].bitcast(F32)[:, 512 * m:512 * (m + 1)].rearrange("p (r w u) -> p r u w", r=2, u=2))
 
-        def job(kind, b, m, eng):
+        def flip(src, m, dst, dst_off, eng, banks=pt):
+            bank = next_bank("pt", banks)
+            for i in range(4):
+                if m is None:
+                    words = src[:, 128 * i:128 * (i + 1)]
+                else:
+                    c0 = 512 * m + 256 * (i // 2)
+                    words = src[:].bitcast(F32)[:, c0 + i % 2:c0 + 256:2]
+                nc.tensor.transpose(bank[:, 128 * i:128 * (i + 1)], words, ident[:])
+            copy_on(eng, dst[:].bitcast(F32)[:, dst_off:dst_off + 512].rearrange("p (a c u) -> p a c u", a=2, u=2),
+                    bank[:].rearrange("p (a u c) -> p a c u", a=2, u=2))
+
+        def job(kind, b, m, eng, banks=pt):
             if kind == "x":
-                flip(x_sb[b], m, xg[b % 2], 256 + 512 * m, eng)
+                if b < LAST:
+                    flip(x_sb[b], m, xg[b % 2], 256 + 512 * m, eng, banks)
+                else:
+                    flip(x_sb[b], m, xg_end, 256 + 1024 * m, eng)
                 return [("x", b, 0)] if m == 1 else []
             if kind == "w":
-                flip(w_sb, m, wg, 512 * m, eng)
+                flip(w_sb, m, wg, 512 * m, eng, banks)
                 return [("w", 0, m // 2)] if m % 2 == 1 else []
-            flip(t_sb[b % NT], m, tg[(2 * b + m // 2) % 4], 512 * (m % 2), eng)
+            if m in PERM_M:
+                flip(tp[(4 * b + m) % 6], None, tg[(2 * b + m // 2) % 4], 512 * (m % 2), eng)
+            else:
+                flip(t_sb[b % NT], m, tg[(2 * b + m // 2) % 4], 512 * (m % 2), eng)
             if m == 3 and b + NT < B:
                 load_t(b + NT)
             return [("t", b, m // 2)] if m % 2 == 1 else []
 
+        ready = set()
+
         def quantise(kind, b, h):
-            if kind == "x":
+            ready.add((kind, b, h))
+            if kind == "x" and b == LAST:
+                g = xg_end
+                for h in range(2):
+                    c = 2048 * h
+                    nc.vector.tensor_copy(out=g[:, c + 4:c + 512], in_=g[:, c + 1024:c + 1532])
+                    nc.vector.tensor_copy(out=g[:, c + 1536:c + 2044], in_=g[:, c + 516:c + 1024])
+                nc.vector.tensor_copy(out=g[:, 2044:2048], in_=g[:, 2560:2564])
+                nc.vector.tensor_copy(out=g[:, 2048:2052], in_=g[:, 1532:1536])
+                quant(xc_end, xs_end, 0, g, 0, 4096)
+            elif kind == "x":
                 g = xg[b % 2]
-                copy_on(HALO, g[:, 2560:3068], g[:, 516:1024])
-                copy_on(HALO, g[:, 4:512], g[:, 2048:2556])
+                nc.vector.tensor_copy(out=g[:, 4:512], in_=g[:, 2048:2556])
+                nc.vector.tensor_copy(out=g[:, 2560:3068], in_=g[:, 516:1024])
                 quant(xc[b % 3], xs[b % 3], 0, g, 0, 2048)
                 quant(xc[b % 3], xs[b % 3], 512, g, 2048, 1024)
             elif kind == "w":
@@ -144,98 +182,154 @@ def tile_bilinearpairedlayer_pb_t_kernel(tc, t_bil, x_r, W_r, b_r, b_bil, out):
             else:
                 quant(tcd[b % 3], tsc[b % 3], 512 * h, tg[(2 * b + h) % 4], 0, 2048)
 
-        def s1(b, t):
-            bank = p1[cnt["p1"] % 2]
-            cnt["p1"] += 1
-            for w, off in ((0, 128), (1, 256), (2, 0)):
+        def hidden(t, bank, c_bank, codes, scales, c_x, width):
+            for w, off in ((2, 0), (0, 128), (1, 256)):
                 s = t * 3 + w
-                nc.tensor.matmul_mx(out=bank[:],
+                nc.tensor.matmul_mx(out=bank[:, c_bank:c_bank + width],
                                     lhsT=wc[:, s * 128:(s + 1) * 128].bitcast(FP8X4),
                                     lhsT_scale=ws[:, s * 128:(s + 1) * 128],
-                                    rhs=xc[b % 3][:, off:off + 512].bitcast(FP8X4),
-                                    rhs_scale=xs[b % 3][:, off:off + 512],
-                                    start=(w == 0), stop=(w == 2))
-            nc.scalar.activation(out=hrt[b % 2][:, t * 512:(t + 1) * 512].rearrange("p (q a) -> p q a", a=4),
-                                 in_=bank[:].rearrange("p (a q) -> p q a", a=4),
+                                    rhs=codes[:, c_x + off:c_x + off + width].bitcast(FP8X4),
+                                    rhs_scale=scales[:, c_x + off:c_x + off + width],
+                                    start=(w == 2), stop=(w == 1))
+
+        def relu(b, t, bank, c_bank, c_out, width):
+            na = width // 128
+            nc.scalar.activation(out=hrt[b % 2][:, c_out:c_out + width].rearrange("p (q a) -> p q a", a=na),
+                                 in_=bank[:, c_bank:c_bank + width].rearrange("p (a q) -> p q a", a=na),
                                  func=ACT.Relu, bias=br[:, t:t + 1], scale=1.0)
 
-        def regroup(b):
-            n = len(RG)
-            dst = hg[b % 2][:].rearrange("p (c t) -> p c t", t=4)
-            src = hrt[b % 2][:].rearrange("p (t c) -> p c t", t=4)
-            for i in range(n):
-                c0 = 512 * i // n
-                c1 = 512 * (i + 1) // n
-                copy_on(RG[i], dst[:, c0:c1], src[:, c0:c1])
-
-        def qh(b):
-            quant(hc[b % 3], hs[b % 3], 0, hg[b % 2], 0, 2048)
-
-        def s2(b, a):
-            if a % 2 == 0:
-                cnt["o"] += 1
-            o = o_sb[(cnt["o"] - 1) % 4]
-            for jh in range(2):
-                bank = p2[cnt["p2"] % 3]
-                cnt["p2"] += 1
-                for k in range(2):
-                    s = 2 * a + k
-                    nc.tensor.matmul_mx(out=bank[:, k * 256:(k + 1) * 256],
-                                        lhsT=tcd[b % 3][:, s * 128:(s + 1) * 128].bitcast(FP8X4),
-                                        lhsT_scale=tsc[b % 3][:, s * 128:(s + 1) * 128],
-                                        rhs=hc[b % 3][:, jh * 256:(jh + 1) * 256].bitcast(FP8X4),
-                                        rhs_scale=hs[b % 3][:, jh * 256:(jh + 1) * 256],
-                                        start=True, stop=True)
-                c0 = (a % 2) * 1024 + jh * 512
-                if a == 3 and jh == 1:
-                    for k in range(2):
-                        nc.scalar.activation(out=o[:, c0:c0 + 512].rearrange("p (j k) -> p j k", k=2)[:, :, k],
-                                             in_=bank[:, k * 256:(k + 1) * 256],
-                                             func=ACT.Identity, bias=bbf[:, k:k + 1], scale=1.0)
+        def s1(b, q):
+            bank = next_bank("p1", p1)
+            h = q // 2
+            done = []
+            for i in range(2):
+                t = 2 * (q % 2) + i
+                if b < LAST:
+                    hidden(t, bank, 256 * i, xc[b % 3], xs[b % 3], 256 * h, 256)
                 else:
-                    nc.vector.tensor_tensor(out=o[:, c0:c0 + 512].rearrange("p (j k) -> p j k", k=2),
-                                            in0=bank[:].rearrange("p (k j) -> p j k", k=2),
-                                            in1=bbt[:].rearrange("p (j k) -> p j k", k=2),
-                                            op=ALU.add)
+                    hidden(t, bank, 256 * i, xc_end, xs_end, 512 * h, 256)
+                done.append((b, t, bank, 256 * i, 1024 * h + 256 * t, 256))
+            return done
+
+        def regroup(b, off, width, engines):
+            n = len(engines)
+            dst = hg[b % 2][:, off:off + width].rearrange("p (c t) -> p c t", t=4)
+            src = hrt[b % 2][:, off:off + width].rearrange("p (t c) -> p c t", t=4)
+            cw = width // 4 // n
+            for i in range(n):
+                copy_on(engines[i], dst[:, cw * i:cw * (i + 1)], src[:, cw * i:cw * (i + 1)])
+
+        def qh(b, off, width):
+            quant(hc[b % 3], hs[b % 3], off // 4, hg[b % 2], off, width)
+            ready.add(("h", b, off // 1024))
+
+        def s2(b, a, jh, bank):
+            for k in range(2):
+                s = 2 * a + k
+                nc.tensor.matmul_mx(out=bank[:, k * 256:(k + 1) * 256],
+                                    lhsT=tcd[b % 3][:, s * 128:(s + 1) * 128].bitcast(FP8X4),
+                                    lhsT_scale=tsc[b % 3][:, s * 128:(s + 1) * 128],
+                                    rhs=hc[b % 3][:, jh * 256:(jh + 1) * 256].bitcast(FP8X4),
+                                    rhs_scale=hs[b % 3][:, jh * 256:(jh + 1) * 256],
+                                    start=True, stop=True)
+            return (b, a, jh, bank)
+
+        def leave(b, a, jh, bank):
+            row = o_sb[(2 * b + a // 2) % 4][:, 1024 * (a % 2):1024 * (a % 2 + 1)]
+            if b < LAST:
+                dst = row.rearrange("p (q h e k) -> p h q e k", h=2, e=2, k=2)[:, jh]
+            else:
+                dst = row.rearrange("p (h q e k) -> p h q e k", h=2, e=2, k=2)[:, jh]
+            if (b, a, jh) in ON_S:
+                for k in range(2):
+                    nc.scalar.activation(out=dst[:, :, :, k],
+                                         in_=bank[:, k * 256:(k + 1) * 256].rearrange("p (q e) -> p q e", e=2),
+                                         func=ACT.Identity, bias=bbf[:, k:k + 1], scale=1.0)
+            else:
+                nc.vector.tensor_tensor(out=dst, in0=bank[:].rearrange("p (k q e) -> p q e k", k=2, e=2),
+                                        in1=bbt[:].rearrange("p (q e k) -> p q e k", e=2, k=2), op=ALU.add)
             o_view = out[b].rearrange("(p a) j k -> p a (j k)", a=4)
-            if b == B - 1:
-                nc.sync.dma_start(out=o_view[:, a, :], in_=o[:, (a % 2) * 1024:(a % 2 + 1) * 1024])
-            elif a % 2 == 1:
+            if b == LAST:
+                nc.sync.dma_start(out=o_view[:, a, 512 * jh:512 * (jh + 1)], in_=row[:, 512 * jh:512 * (jh + 1)])
+            elif a % 2 == 1 and jh == 1:
+                o = o_sb[(2 * b + a // 2) % 4]
                 nc.sync.dma_start(out=o_view[:, a - 1:a + 1, :], in_=o[:].rearrange("p (a r) -> p a r", a=2))
 
-        jobs = [("x", 0, 0), ("x", 0, 1)] + [("w", 0, m) for m in range(6)] + [("x", 1, 0), ("x", 1, 1)]
+        def spread_b_bil():
+            bank = next_bank("p2", p2)
+            nc.tensor.matmul(out=bank[:, 0:2], lhsT=ones[:], rhs=rows[:], start=True, stop=True)
+            nc.vector.tensor_copy(out=bbf[:], in_=bank[:, 0:2])
+            nc.vector.tensor_copy(out=bbt[:].rearrange("p (j k) -> p j k", k=2),
+                                  in_=bbf[:].unsqueeze(1).to_broadcast([P, 256, 2]))
+
+        jobs = [("x", 0, 0), ("x", 0, 1)] + [("w", 0, m) for m in range(6)]
+        head = 8
         for b in range(B):
-            if b + 2 < B:
-                jobs += [("x", b + 2, 0), ("x", b + 2, 1)]
-            jobs += [("t", b, m) for m in range(4)]
+            jobs += [("t", b, 0), ("t", b, 1)]
+            if b < LAST:
+                jobs += [("x", b + 1, 0), ("x", b + 1, 1)]
+            jobs += [("t", b, 2), ("t", b, 3)]
         todo = []
-        for i in range(8 + AHEAD):
-            ready = todo
-            kind, b, m = jobs[i]
-            todo = job(kind, b, m, "v" if i % 2 else "s")
-            for kind, b, h in ready:
-                quantise(kind, b, h)
-        for kind, b, h in todo:
-            quantise(kind, b, h)
-        nxt = 8 + AHEAD
-        waiting = []
-        for tick in range(4 * B + LAG):
+        for i in range(head):
+            todo += job(jobs[i][0], jobs[i][1], jobs[i][2], HEAD[i], pt + p2)
+            if i in (3, 5):
+                for item in todo:
+                    quantise(item[0], item[1], item[2])
+                todo = []
+        waiting = [(0, item) for item in todo]
+        nc.vector.tensor_copy(out=br[:], in_=br_bf[:])
+        nxt = head
+        plans = [2 if tick in EXTRA else SLOTS[min(tick // 4, 1)][tick % 4] for tick in range(4 * B)] + [0]
+        cnt["perm"] = 0
+
+        def permute_some(tick):
+            for kind, b, m in jobs[nxt:nxt + plans[tick + 1]]:
+                while kind == "t" and cnt["perm"] < 4 * b + m + 1:
+                    permute(cnt["perm"] // 4, cnt["perm"] % 4)
+                    cnt["perm"] += 1
+
+        scores = [(b, a, jh) for b in range(B) for jh in range(2) for a in range(4)]
+        full1 = []
+        full2 = []
+        for tick in range(4 * B):
             n = tick // 4
             q = tick % 4
-            if q == 0 and 1 <= n <= B:
-                regroup(n - 1)
-            for i in range(PLAN[q]):
-                if nxt < len(jobs):
-                    kind, b, m = jobs[nxt]
-                    nxt += 1
-                    waiting += [(tick + QDELAY, item) for item in job(kind, b, m, "s")]
-            if n < B:
-                s1(n, q)
-            if tick >= LAG:
-                s2((tick - LAG) // 4, (tick - LAG) % 4)
-            if q == QHQ and 1 <= n <= B:
-                qh(n - 1)
-            for due, item in waiting:
-                if due <= tick:
+            for item in full1:
+                relu(item[0], item[1], item[2], item[3], item[4], item[5])
+            for item in full2:
+                leave(item[0], item[1], item[2], item[3])
+            full2 = []
+            for kind, b, m in jobs[nxt:nxt + plans[tick]]:
+                waiting += [(tick + QD[kind], item) for item in job(kind, b, m, "s")]
+            nxt += plans[tick]
+            full1 = s1(n, q)
+            if tick == BTICK:
+                spread_b_bil()
+            for b, a, jh in scores[0:2 if tick < 4 * LAST else 4]:
+                if ("h", b, jh) in ready and ("t", b, a // 2) in ready:
+                    full2.append(s2(b, a, jh, next_bank("p2", p2)))
+                else:
+                    break
+            scores = scores[len(full2):]
+            if tick >= 2 and q % 2 == 0:
+                b, h = (tick - 2) // 4, (tick - 2) % 4 // 2
+                regroup(b, 1024 * h, 1024, RG)
+                qh(b, 1024 * h, 1024)
+            for when, item in waiting:
+                if when <= tick or tick < 1:
                     quantise(item[0], item[1], item[2])
-            waiting = [(due, item) for due, item in waiting if due > tick]
+            waiting = [(when, item) for when, item in waiting if when > tick and tick >= 1]
+            permute_some(tick)
+        for item in full1:
+            relu(item[0], item[1], item[2], item[3], item[4], item[5])
+        assert scores == [(LAST, a, 1) for a in range(4)] and len(full2) == 4
+        for item in full2[0:3:2]:
+            leave(item[0], item[1], item[2], item[3])
+        regroup(LAST, 1024, 1024, RG_END)
+        qh(LAST, 1024, 1024)
+        for item in full2[1:4:2]:
+            leave(item[0], item[1], item[2], item[3])
+        banks = [p1[0], pt[0], pt[1], p2[0]]
+        full2 = [s2(LAST, a, 1, banks[a]) for a in range(4)]
+        for item in full2:
+            leave(item[0], item[1], item[2], item[3])

@@ -19,7 +19,6 @@ FLOPS = 2 * 8 * 512 * 512 * 1536 + 2 * 8 * 1024 * 512 * 512
 BANKS_T, BANKS_1, BANKS_2 = 2, 2, 4
 HEAD = "vsvsssss"
 BTICK = 2
-PERM_M = ()
 QD = {"x": 1, "t": 1, "w": 0}
 SLOTS = ((0, 2, 2, 2), (2, 2, 0, 2))
 RG = ("v", "s")
@@ -45,10 +44,6 @@ def tile_bilinearpairedlayer_pb_t_kernel(tc, t_bil, x_r, W_r, b_r, b_bil, out):
         xg = [sb.tile([P, 3072], BF16, name="xg%d" % i, align_bytes=64) for i in range(2)]
         xc = [sb.tile([P, 768], U32, name="xc%d" % i, align_bytes=64) for i in range(3)]
         xs = [sb.tile([P, 768], U8, name="xs%d" % i, align_bytes=64) for i in range(3)]
-        xg_end = sb.tile([P, 4096], BF16, name="xg_end", align_bytes=64)
-        xc_end = sb.tile([P, 1024], U32, name="xc_end", align_bytes=64)
-        xs_end = sb.tile([P, 1024], U8, name="xs_end", align_bytes=64)
-        tp = [sb.tile([P, 512], F32, name="tp%d" % i) for i in range(6)]
         tg = [sb.tile([P, 2048], BF16, name="tg%d" % i, align_bytes=64) for i in range(4)]
         tcd = [sb.tile([P, 1024], U32, name="tcd%d" % i, align_bytes=64) for i in range(3)]
         tsc = [sb.tile([P, 1024], U8, name="tsc%d" % i, align_bytes=64) for i in range(3)]
@@ -72,21 +67,15 @@ def tile_bilinearpairedlayer_pb_t_kernel(tc, t_bil, x_r, W_r, b_r, b_bil, out):
         ctx.enter_context(tc.manual_schedule())
 
         def load_x(b):
-            if b < LAST:
-                nc.sync.dma_start(out=x_sb[b][:], in_=x_r[b].rearrange("(p a) f -> p (a f)", a=4))
-            else:
-                nc.sync.dma_start(out=x_sb[b][:].rearrange("p (h r) -> p h r", h=2),
-                                  in_=x_r[b].rearrange("(h p a) f -> p h (a f)", h=2, a=2))
+            nc.sync.dma_start(out=x_sb[b][:], in_=x_r[b].rearrange("(p a) f -> p (a f)", a=4))
 
         def load_t(b):
             nc.sync.dma_start(out=t_sb[b % NT][:], in_=t_bil[b].rearrange("(p a) k g -> p (a k g)", a=4))
 
-        x0_view = x_r[0].rearrange("(p a) f -> p (a f)", a=4)
-        for h in range(2):
-            nc.sync.dma_start(out=x_sb[0][:, 1024 * h:1024 * (h + 1)], in_=x0_view[:, 1024 * h:1024 * (h + 1)])
+        load_x(0)
         w_view = W_r.rearrange("(p t) f -> p (t f)", t=4)
-        for m in range(6):
-            nc.sync.dma_start(out=w_sb[:, 1024 * m:1024 * (m + 1)], in_=w_view[:, 1024 * m:1024 * (m + 1)])
+        for m in range(3):
+            nc.sync.dma_start(out=w_sb[:, 2048 * m:2048 * (m + 1)], in_=w_view[:, 2048 * m:2048 * (m + 1)])
         with nc.allow_non_contiguous_dma(reason="four bfloat16 of b_r to a partition"):
             nc.scalar.dma_start(out=br_bf[:], in_=b_r.rearrange("(p t) -> p t", t=4))
         nc.vector.memset(rows[:], 0.0)
@@ -104,8 +93,6 @@ def tile_bilinearpairedlayer_pb_t_kernel(tc, t_bil, x_r, W_r, b_r, b_bil, out):
         for i in range(2):
             nc.vector.memset(xg[i][:, 0:4], 0.0)
             nc.vector.memset(xg[i][:, 3068:3072], 0.0)
-        nc.vector.memset(xg_end[:, 0:4], 0.0)
-        nc.vector.memset(xg_end[:, 4092:4096], 0.0)
 
         def next_bank(which, banks):
             bank = banks[cnt[which] % len(banks)]
@@ -123,58 +110,43 @@ def tile_bilinearpairedlayer_pb_t_kernel(tc, t_bil, x_r, W_r, b_r, b_bil, out):
                                   scales=scales[:, c_off:c_off + width // 4],
                                   in_=src[:, s_off:s_off + width])
 
-        def permute(b, m):
-            if m in PERM_M:
-                nc.scalar.copy(out=tp[(4 * b + m) % 6][:].rearrange("p (r u w) -> p r u w", r=2, u=2),
-                               in_=t_sb[b % NT][:].bitcast(F32)[:, 512 * m:512 * (m + 1)].rearrange("p (r w u) -> p r u w", r=2, u=2))
-
-        def flip(src, m, dst, dst_off, eng, banks=pt):
+        def transposed(src, m, banks):
             bank = next_bank("pt", banks)
             for i in range(4):
-                if m is None:
-                    words = src[:, 128 * i:128 * (i + 1)]
-                else:
-                    c0 = 512 * m + 256 * (i // 2)
-                    words = src[:].bitcast(F32)[:, c0 + i % 2:c0 + 256:2]
-                nc.tensor.transpose(bank[:, 128 * i:128 * (i + 1)], words, ident[:])
-            copy_on(eng, dst[:].bitcast(F32)[:, dst_off:dst_off + 512].rearrange("p (a c u) -> p a c u", a=2, u=2),
-                    bank[:].rearrange("p (a u c) -> p a c u", a=2, u=2))
+                c0 = 512 * m + 256 * (i // 2)
+                nc.tensor.transpose(bank[:, 128 * i:128 * (i + 1)], src[:].bitcast(F32)[:, c0 + i % 2:c0 + 256:2], ident[:])
+            return bank
 
         def job(kind, b, m, eng, banks=pt):
             if kind == "x":
-                if b < LAST:
-                    flip(x_sb[b], m, xg[b % 2], 256 + 512 * m, eng, banks)
-                else:
-                    flip(x_sb[b], m, xg_end, 256 + 1024 * m, eng)
+                bank = transposed(x_sb[b], m, banks)
+                dst = xg[b % 2][:].bitcast(F32).rearrange("p (h a c u) -> p h a c u", h=2, a=6, u=2)
+                src = bank[:].rearrange("p (a u h c) -> p h a c u", a=2, u=2, h=2)
+                for h in range(2):
+                    copy_on(eng, dst[:, h, 1 + 2 * m:3 + 2 * m], src[:, h])
                 return [("x", b, 0)] if m == 1 else []
             if kind == "w":
-                flip(w_sb, m, wg, 512 * m, eng, banks)
-                return [("w", 0, m // 2)] if m % 2 == 1 else []
-            if m in PERM_M:
-                flip(tp[(4 * b + m) % 6], None, tg[(2 * b + m // 2) % 4], 512 * (m % 2), eng)
+                src, dst, c0 = w_sb, wg, 512 * m
             else:
-                flip(t_sb[b % NT], m, tg[(2 * b + m // 2) % 4], 512 * (m % 2), eng)
-            if m == 3 and b + NT < B:
+                src, dst, c0 = t_sb[b % NT], tg[(2 * b + m // 2) % 4], 512 * (m % 2)
+            bank = transposed(src, m, banks)
+            copy_on(eng, dst[:].bitcast(F32)[:, c0:c0 + 512].rearrange("p (a c u) -> p a c u", a=2, u=2),
+                    bank[:].rearrange("p (a u c) -> p a c u", a=2, u=2))
+            if kind == "t" and m == 3 and b + NT < B:
                 load_t(b + NT)
-            return [("t", b, m // 2)] if m % 2 == 1 else []
+            return [(kind, b, m // 2)] if m % 2 == 1 else []
 
         ready = set()
 
         def quantise(kind, b, h):
             ready.add((kind, b, h))
-            if kind == "x" and b == LAST:
-                g = xg_end
-                for h in range(2):
-                    c = 2048 * h
-                    nc.vector.tensor_copy(out=g[:, c + 4:c + 512], in_=g[:, c + 1024:c + 1532])
-                    nc.vector.tensor_copy(out=g[:, c + 1536:c + 2044], in_=g[:, c + 516:c + 1024])
-                nc.vector.tensor_copy(out=g[:, 2044:2048], in_=g[:, 2560:2564])
-                nc.vector.tensor_copy(out=g[:, 2048:2052], in_=g[:, 1532:1536])
-                quant(xc_end, xs_end, 0, g, 0, 4096)
-            elif kind == "x":
+            if kind == "x":
                 g = xg[b % 2]
-                nc.vector.tensor_copy(out=g[:, 4:512], in_=g[:, 2048:2556])
-                nc.vector.tensor_copy(out=g[:, 2560:3068], in_=g[:, 516:1024])
+                gh = g[:].rearrange("p (h c) -> p h c", h=2)
+                nc.vector.tensor_copy(out=gh[:, :, 4:256], in_=gh[:, :, 1024:1276])
+                nc.vector.tensor_copy(out=gh[:, :, 1280:1532], in_=gh[:, :, 260:512])
+                nc.vector.tensor_copy(out=g[:, 1536:1540], in_=g[:, 1276:1280])
+                nc.vector.tensor_copy(out=g[:, 1532:1536], in_=g[:, 1792:1796])
                 quant(xc[b % 3], xs[b % 3], 0, g, 0, 2048)
                 quant(xc[b % 3], xs[b % 3], 512, g, 2048, 1024)
             elif kind == "w":
@@ -183,7 +155,7 @@ def tile_bilinearpairedlayer_pb_t_kernel(tc, t_bil, x_r, W_r, b_r, b_bil, out):
                 quant(tcd[b % 3], tsc[b % 3], 512 * h, tg[(2 * b + h) % 4], 0, 2048)
 
         def hidden(t, bank, c_bank, codes, scales, c_x, width):
-            for w, off in ((2, 0), (0, 128), (1, 256)):
+            for w, off in ((2, 0), (0, 64), (1, 128)):
                 s = t * 3 + w
                 nc.tensor.matmul_mx(out=bank[:, c_bank:c_bank + width],
                                     lhsT=wc[:, s * 128:(s + 1) * 128].bitcast(FP8X4),
@@ -193,9 +165,8 @@ def tile_bilinearpairedlayer_pb_t_kernel(tc, t_bil, x_r, W_r, b_r, b_bil, out):
                                     start=(w == 2), stop=(w == 1))
 
         def relu(b, t, bank, c_bank, c_out, width):
-            na = width // 128
-            nc.scalar.activation(out=hrt[b % 2][:, c_out:c_out + width].rearrange("p (q a) -> p q a", a=na),
-                                 in_=bank[:, c_bank:c_bank + width].rearrange("p (a q) -> p q a", a=na),
+            nc.scalar.activation(out=hrt[b % 2][:, c_out:c_out + width].rearrange("p (q a) -> p q a", a=4),
+                                 in_=bank[:, c_bank:c_bank + width].rearrange("p (a q) -> p q a", a=4),
                                  func=ACT.Relu, bias=br[:, t:t + 1], scale=1.0)
 
         def s1(b, q):
@@ -204,10 +175,7 @@ def tile_bilinearpairedlayer_pb_t_kernel(tc, t_bil, x_r, W_r, b_r, b_bil, out):
             done = []
             for i in range(2):
                 t = 2 * (q % 2) + i
-                if b < LAST:
-                    hidden(t, bank, 256 * i, xc[b % 3], xs[b % 3], 256 * h, 256)
-                else:
-                    hidden(t, bank, 256 * i, xc_end, xs_end, 512 * h, 256)
+                hidden(t, bank, 256 * i, xc[b % 3], xs[b % 3], 384 * h, 256)
                 done.append((b, t, bank, 256 * i, 1024 * h + 256 * t, 256))
             return done
 
@@ -236,18 +204,14 @@ def tile_bilinearpairedlayer_pb_t_kernel(tc, t_bil, x_r, W_r, b_r, b_bil, out):
 
         def leave(b, a, jh, bank):
             row = o_sb[(2 * b + a // 2) % 4][:, 1024 * (a % 2):1024 * (a % 2 + 1)]
-            if b < LAST:
-                dst = row.rearrange("p (q h e k) -> p h q e k", h=2, e=2, k=2)[:, jh]
-            else:
-                dst = row.rearrange("p (h q e k) -> p h q e k", h=2, e=2, k=2)[:, jh]
+            dst = row[:, 512 * jh:512 * (jh + 1)].rearrange("p (j k) -> p j k", k=2)
             if (b, a, jh) in ON_S:
                 for k in range(2):
-                    nc.scalar.activation(out=dst[:, :, :, k],
-                                         in_=bank[:, k * 256:(k + 1) * 256].rearrange("p (q e) -> p q e", e=2),
+                    nc.scalar.activation(out=dst[:, :, k], in_=bank[:, k * 256:(k + 1) * 256],
                                          func=ACT.Identity, bias=bbf[:, k:k + 1], scale=1.0)
             else:
-                nc.vector.tensor_tensor(out=dst, in0=bank[:].rearrange("p (k q e) -> p q e k", k=2, e=2),
-                                        in1=bbt[:].rearrange("p (q e k) -> p q e k", e=2, k=2), op=ALU.add)
+                nc.vector.tensor_tensor(out=dst, in0=bank[:].rearrange("p (k j) -> p j k", k=2),
+                                        in1=bbt[:].rearrange("p (j k) -> p j k", k=2), op=ALU.add)
             o_view = out[b].rearrange("(p a) j k -> p a (j k)", a=4)
             if b == LAST:
                 nc.sync.dma_start(out=o_view[:, a, 512 * jh:512 * (jh + 1)], in_=row[:, 512 * jh:512 * (jh + 1)])
@@ -280,14 +244,6 @@ def tile_bilinearpairedlayer_pb_t_kernel(tc, t_bil, x_r, W_r, b_r, b_bil, out):
         nc.vector.tensor_copy(out=br[:], in_=br_bf[:])
         nxt = head
         plans = [2 if tick in EXTRA else SLOTS[min(tick // 4, 1)][tick % 4] for tick in range(4 * B)] + [0]
-        cnt["perm"] = 0
-
-        def permute_some(tick):
-            for kind, b, m in jobs[nxt:nxt + plans[tick + 1]]:
-                while kind == "t" and cnt["perm"] < 4 * b + m + 1:
-                    permute(cnt["perm"] // 4, cnt["perm"] % 4)
-                    cnt["perm"] += 1
-
         scores = [(b, a, jh) for b in range(B) for jh in range(2) for a in range(4)]
         full1 = []
         full2 = []
@@ -319,7 +275,6 @@ def tile_bilinearpairedlayer_pb_t_kernel(tc, t_bil, x_r, W_r, b_r, b_bil, out):
                 if when <= tick or tick < 1:
                     quantise(item[0], item[1], item[2])
             waiting = [(when, item) for when, item in waiting if when > tick and tick >= 1]
-            permute_some(tick)
         for item in full1:
             relu(item[0], item[1], item[2], item[3], item[4], item[5])
         assert scores == [(LAST, a, 1) for a in range(4)] and len(full2) == 4

@@ -22,9 +22,12 @@ BTICK = 2
 QD = {"x": 1, "t": 1, "w": 0}
 SLOTS = ((0, 2, 2, 2), (2, 2, 0, 2))
 RG = ("v", "s")
+RG_ALL = ("v", "s")
 RG_END = ("v", "s")
-ON_S = ((7, 1, 0), (7, 3, 0), (7, 1, 1))
+ON_S = ((6, 3, 1), (7, 1, 0), (7, 1, 1))
 NT = 4
+SPLIT = 6
+S_CAP = (2, 2, 4)
 EXTRA = ()
 
 
@@ -120,9 +123,10 @@ def tile_bilinearpairedlayer_pb_t_kernel(tc, t_bil, x_r, W_r, b_r, b_bil, out):
         def job(kind, b, m, eng, banks=pt):
             if kind == "x":
                 bank = transposed(x_sb[b], m, banks)
-                dst = xg[b % 2][:].bitcast(F32).rearrange("p (h a c u) -> p h a c u", h=2, a=6, u=2)
-                src = bank[:].rearrange("p (a u h c) -> p h a c u", a=2, u=2, h=2)
-                for h in range(2):
+                nh = 1 if b < SPLIT else 2
+                dst = xg[b % 2][:].bitcast(F32).rearrange("p (h a c u) -> p h a c u", h=nh, a=6, u=2)
+                src = bank[:].rearrange("p (a u h c) -> p h a c u", a=2, u=2, h=nh)
+                for h in range(nh):
                     copy_on(eng, dst[:, h, 1 + 2 * m:3 + 2 * m], src[:, h])
                 return [("x", b, 0)] if m == 1 else []
             if kind == "w":
@@ -142,11 +146,15 @@ def tile_bilinearpairedlayer_pb_t_kernel(tc, t_bil, x_r, W_r, b_r, b_bil, out):
             ready.add((kind, b, h))
             if kind == "x":
                 g = xg[b % 2]
-                gh = g[:].rearrange("p (h c) -> p h c", h=2)
-                nc.vector.tensor_copy(out=gh[:, :, 4:256], in_=gh[:, :, 1024:1276])
-                nc.vector.tensor_copy(out=gh[:, :, 1280:1532], in_=gh[:, :, 260:512])
-                nc.vector.tensor_copy(out=g[:, 1536:1540], in_=g[:, 1276:1280])
-                nc.vector.tensor_copy(out=g[:, 1532:1536], in_=g[:, 1792:1796])
+                if b < SPLIT:
+                    nc.vector.tensor_copy(out=g[:, 4:512], in_=g[:, 2048:2556])
+                    nc.vector.tensor_copy(out=g[:, 2560:3068], in_=g[:, 516:1024])
+                else:
+                    gh = g[:].rearrange("p (h c) -> p h c", h=2)
+                    nc.vector.tensor_copy(out=gh[:, :, 4:256], in_=gh[:, :, 1024:1276])
+                    nc.vector.tensor_copy(out=gh[:, :, 1280:1532], in_=gh[:, :, 260:512])
+                    nc.vector.tensor_copy(out=g[:, 1536:1540], in_=g[:, 1276:1280])
+                    nc.vector.tensor_copy(out=g[:, 1532:1536], in_=g[:, 1792:1796])
                 quant(xc[b % 3], xs[b % 3], 0, g, 0, 2048)
                 quant(xc[b % 3], xs[b % 3], 512, g, 2048, 1024)
             elif kind == "w":
@@ -155,7 +163,8 @@ def tile_bilinearpairedlayer_pb_t_kernel(tc, t_bil, x_r, W_r, b_r, b_bil, out):
                 quant(tcd[b % 3], tsc[b % 3], 512 * h, tg[(2 * b + h) % 4], 0, 2048)
 
         def hidden(t, bank, c_bank, codes, scales, c_x, width):
-            for w, off in ((2, 0), (0, 64), (1, 128)):
+            step = width // 4
+            for w, off in ((2, 0), (0, step), (1, 2 * step)):
                 s = t * 3 + w
                 nc.tensor.matmul_mx(out=bank[:, c_bank:c_bank + width],
                                     lhsT=wc[:, s * 128:(s + 1) * 128].bitcast(FP8X4),
@@ -171,6 +180,9 @@ def tile_bilinearpairedlayer_pb_t_kernel(tc, t_bil, x_r, W_r, b_r, b_bil, out):
 
         def s1(b, q):
             bank = next_bank("p1", p1)
+            if b < SPLIT:
+                hidden(q, bank, 0, xc[b % 3], xs[b % 3], 0, 512)
+                return [(b, q, bank, 0, 512 * q, 512)]
             h = q // 2
             done = []
             for i in range(2):
@@ -244,7 +256,8 @@ def tile_bilinearpairedlayer_pb_t_kernel(tc, t_bil, x_r, W_r, b_r, b_bil, out):
         nc.vector.tensor_copy(out=br[:], in_=br_bf[:])
         nxt = head
         plans = [2 if tick in EXTRA else SLOTS[min(tick // 4, 1)][tick % 4] for tick in range(4 * B)] + [0]
-        scores = [(b, a, jh) for b in range(B) for jh in range(2) for a in range(4)]
+        scores = [(b, a, jh) for b in range(SPLIT) for a in range(4) for jh in range(2)]
+        scores += [(b, a, jh) for b in range(SPLIT, B) for jh in range(2) for a in range(4)]
         full1 = []
         full2 = []
         for tick in range(4 * B):
@@ -261,7 +274,7 @@ def tile_bilinearpairedlayer_pb_t_kernel(tc, t_bil, x_r, W_r, b_r, b_bil, out):
             full1 = s1(n, q)
             if tick == BTICK:
                 spread_b_bil()
-            for b, a, jh in scores[0:2 if tick < 4 * LAST else 4]:
+            for b, a, jh in scores[0:S_CAP[0] if n < SPLIT else S_CAP[1] if n < LAST else S_CAP[2]]:
                 if ("h", b, jh) in ready and ("t", b, a // 2) in ready:
                     full2.append(s2(b, a, jh, next_bank("p2", p2)))
                 else:
@@ -269,8 +282,13 @@ def tile_bilinearpairedlayer_pb_t_kernel(tc, t_bil, x_r, W_r, b_r, b_bil, out):
             scores = scores[len(full2):]
             if tick >= 2 and q % 2 == 0:
                 b, h = (tick - 2) // 4, (tick - 2) % 4 // 2
-                regroup(b, 1024 * h, 1024, RG)
-                qh(b, 1024 * h, 1024)
+                if b >= SPLIT:
+                    regroup(b, 1024 * h, 1024, RG)
+                    qh(b, 1024 * h, 1024)
+                elif h == 1:
+                    regroup(b, 0, 2048, RG_ALL)
+                    qh(b, 0, 1024)
+                    qh(b, 1024, 1024)
             for when, item in waiting:
                 if when <= tick or tick < 1:
                     quantise(item[0], item[1], item[2])

@@ -22,10 +22,13 @@ BTICK = 2
 QD = {"x": 1, "t": 1, "w": 0}
 SLOTS = ((0, 2, 2, 2), (2, 2, 0, 2))
 RG = ("v", "s")
-RG_ALL = ("v", "s")
+RG_ALL = ("v", "g", "g")
 RG_END = ("v", "s")
-ON_S = ((6, 3, 1), (7, 1, 0), (7, 1, 1))
+ON_S = ((6, 3, 0), (6, 3, 1), (7, 1, 0), (7, 1, 1))
 NT = 4
+PERM_M = (0, 2)
+PERM_LEAD = 2
+PERM_POS = "end"
 SPLIT = 6
 S_CAP = (2, 2, 4)
 EXTRA = ()
@@ -47,6 +50,7 @@ def tile_bilinearpairedlayer_pb_t_kernel(tc, t_bil, x_r, W_r, b_r, b_bil, out):
         xg = [sb.tile([P, 3072], BF16, name="xg%d" % i, align_bytes=64) for i in range(2)]
         xc = [sb.tile([P, 768], U32, name="xc%d" % i, align_bytes=64) for i in range(3)]
         xs = [sb.tile([P, 768], U8, name="xs%d" % i, align_bytes=64) for i in range(3)]
+        tp = [sb.tile([P, 512], F32, name="tp%d" % i) for i in range(4)]
         tg = [sb.tile([P, 2048], BF16, name="tg%d" % i, align_bytes=64) for i in range(4)]
         tcd = [sb.tile([P, 1024], U32, name="tcd%d" % i, align_bytes=64) for i in range(3)]
         tsc = [sb.tile([P, 1024], U8, name="tsc%d" % i, align_bytes=64) for i in range(3)]
@@ -105,13 +109,25 @@ def tile_bilinearpairedlayer_pb_t_kernel(tc, t_bil, x_r, W_r, b_r, b_bil, out):
         def copy_on(eng, o_ap, i_ap):
             if eng == "v":
                 nc.vector.tensor_copy(out=o_ap, in_=i_ap)
-            else:
+            elif eng == "s":
                 nc.scalar.copy(out=o_ap, in_=i_ap)
+            else:
+                nc.gpsimd.tensor_scalar(out=o_ap, in0=i_ap, scalar1=1.0, scalar2=0.0, op0=ALU.mult, op1=ALU.add)
 
         def quant(codes, scales, c_off, src, s_off, width):
             nc.vector.quantize_mx(out=codes[:, c_off:c_off + width // 4].bitcast(FP8X4),
                                   scales=scales[:, c_off:c_off + width // 4],
                                   in_=src[:, s_off:s_off + width])
+
+        def permute(b, m):
+            nc.scalar.copy(out=tp[(4 * b + m) % 4][:].rearrange("p (r u w) -> p r u w", r=2, u=2),
+                           in_=t_sb[b % NT][:].bitcast(F32)[:, 512 * m:512 * (m + 1)].rearrange("p (r w u) -> p r u w", r=2, u=2))
+
+        def transposed_plain(src, banks):
+            bank = next_bank("pt", banks)
+            for i in range(4):
+                nc.tensor.transpose(bank[:, 128 * i:128 * (i + 1)], src[:, 128 * i:128 * (i + 1)], ident[:])
+            return bank
 
         def transposed(src, m, banks):
             bank = next_bank("pt", banks)
@@ -133,7 +149,10 @@ def tile_bilinearpairedlayer_pb_t_kernel(tc, t_bil, x_r, W_r, b_r, b_bil, out):
                 src, dst, c0 = w_sb, wg, 512 * m
             else:
                 src, dst, c0 = t_sb[b % NT], tg[(2 * b + m // 2) % 4], 512 * (m % 2)
-            bank = transposed(src, m, banks)
+            if kind == "t" and m in PERM_M:
+                bank = transposed_plain(tp[(4 * b + m) % 4], banks)
+            else:
+                bank = transposed(src, m, banks)
             copy_on(eng, dst[:].bitcast(F32)[:, c0:c0 + 512].rearrange("p (a c u) -> p a c u", a=2, u=2),
                     bank[:].rearrange("p (a u c) -> p a c u", a=2, u=2))
             if kind == "t" and m == 3 and b + NT < B:
@@ -195,9 +214,10 @@ def tile_bilinearpairedlayer_pb_t_kernel(tc, t_bil, x_r, W_r, b_r, b_bil, out):
             n = len(engines)
             dst = hg[b % 2][:, off:off + width].rearrange("p (c t) -> p c t", t=4)
             src = hrt[b % 2][:, off:off + width].rearrange("p (t c) -> p c t", t=4)
-            cw = width // 4 // n
+            blocks = width // 64
             for i in range(n):
-                copy_on(engines[i], dst[:, cw * i:cw * (i + 1)], src[:, cw * i:cw * (i + 1)])
+                c0, c1 = blocks * i // n * 16, blocks * (i + 1) // n * 16
+                copy_on(engines[i], dst[:, c0:c1], src[:, c0:c1])
 
         def qh(b, off, width):
             quant(hc[b % 3], hs[b % 3], off // 4, hg[b % 2], off, width)
@@ -256,6 +276,15 @@ def tile_bilinearpairedlayer_pb_t_kernel(tc, t_bil, x_r, W_r, b_r, b_bil, out):
         nc.vector.tensor_copy(out=br[:], in_=br_bf[:])
         nxt = head
         plans = [2 if tick in EXTRA else SLOTS[min(tick // 4, 1)][tick % 4] for tick in range(4 * B)] + [0]
+        cnt["perm"] = head
+
+        def permute_ahead(tick):
+            upto = nxt + sum(plans[tick + 1:tick + 1 + PERM_LEAD])
+            for kind, b, m in jobs[cnt["perm"]:upto]:
+                if kind == "t" and m in PERM_M:
+                    permute(b, m)
+            cnt["perm"] = max(cnt["perm"], min(upto, len(jobs)))
+
         scores = [(b, a, jh) for b in range(SPLIT) for a in range(4) for jh in range(2)]
         scores += [(b, a, jh) for b in range(SPLIT, B) for jh in range(2) for a in range(4)]
         full1 = []
@@ -272,6 +301,8 @@ def tile_bilinearpairedlayer_pb_t_kernel(tc, t_bil, x_r, W_r, b_r, b_bil, out):
                 waiting += [(tick + QD[kind], item) for item in job(kind, b, m, "s")]
             nxt += plans[tick]
             full1 = s1(n, q)
+            if PERM_POS == "mid":
+                permute_ahead(tick)
             if tick == BTICK:
                 spread_b_bil()
             for b, a, jh in scores[0:S_CAP[0] if n < SPLIT else S_CAP[1] if n < LAST else S_CAP[2]]:
@@ -293,6 +324,8 @@ def tile_bilinearpairedlayer_pb_t_kernel(tc, t_bil, x_r, W_r, b_r, b_bil, out):
                 if when <= tick or tick < 1:
                     quantise(item[0], item[1], item[2])
             waiting = [(when, item) for when, item in waiting if when > tick and tick >= 1]
+            if PERM_POS == "end":
+                permute_ahead(tick)
         for item in full1:
             relu(item[0], item[1], item[2], item[3], item[4], item[5])
         assert scores == [(LAST, a, 1) for a in range(4)] and len(full2) == 4

@@ -21,14 +21,18 @@ HEAD = "vsvsssss"
 BTICK = 2
 QD = {"x": 1, "t": 1, "w": 0}
 SLOTS = ((0, 2, 2, 2), (2, 2, 0, 2))
-RG = ("v", "s")
-RG_ALL = ("v", "g", "g")
-RG_END = ("v", "s")
-ON_S = ((6, 3, 0), (6, 3, 1), (7, 1, 0), (7, 1, 1))
+RG = ("g", "v")
+RG_ALL = ("v", "g", "s")
+RG_END = ("v",)
+ON_S = ((5, 1, 0), (5, 3, 0), (6, 3, 0), (6, 3, 1), (7, 2, 0), (7, 2, 1))
 NT = 4
-PERM_M = (0, 2)
+PERM_M = ()
+FINE = 6
+ROWS = 6
+PERM_E = "ssss"
+PERM_X = ()
 PERM_LEAD = 2
-PERM_POS = "end"
+ORDER = "ULFACRQP"
 SPLIT = 6
 S_CAP = (2, 2, 4)
 EXTRA = ()
@@ -51,6 +55,7 @@ def tile_bilinearpairedlayer_pb_t_kernel(tc, t_bil, x_r, W_r, b_r, b_bil, out):
         xc = [sb.tile([P, 768], U32, name="xc%d" % i, align_bytes=64) for i in range(3)]
         xs = [sb.tile([P, 768], U8, name="xs%d" % i, align_bytes=64) for i in range(3)]
         tp = [sb.tile([P, 512], F32, name="tp%d" % i) for i in range(4)]
+        xp = [sb.tile([P, 512], F32, name="xp%d" % i) for i in range(2)]
         tg = [sb.tile([P, 2048], BF16, name="tg%d" % i, align_bytes=64) for i in range(4)]
         tcd = [sb.tile([P, 1024], U32, name="tcd%d" % i, align_bytes=64) for i in range(3)]
         tsc = [sb.tile([P, 1024], U8, name="tsc%d" % i, align_bytes=64) for i in range(3)]
@@ -119,9 +124,9 @@ def tile_bilinearpairedlayer_pb_t_kernel(tc, t_bil, x_r, W_r, b_r, b_bil, out):
                                   scales=scales[:, c_off:c_off + width // 4],
                                   in_=src[:, s_off:s_off + width])
 
-        def permute(b, m):
-            nc.scalar.copy(out=tp[(4 * b + m) % 4][:].rearrange("p (r u w) -> p r u w", r=2, u=2),
-                           in_=t_sb[b % NT][:].bitcast(F32)[:, 512 * m:512 * (m + 1)].rearrange("p (r w u) -> p r u w", r=2, u=2))
+        def permute(src, dst, m, eng):
+            copy_on(eng, dst[:].rearrange("p (r u w) -> p r u w", r=2, u=2),
+                    src[:].bitcast(F32)[:, 512 * m:512 * (m + 1)].rearrange("p (r w u) -> p r u w", r=2, u=2))
 
         def transposed_plain(src, banks):
             bank = next_bank("pt", banks)
@@ -138,7 +143,7 @@ def tile_bilinearpairedlayer_pb_t_kernel(tc, t_bil, x_r, W_r, b_r, b_bil, out):
 
         def job(kind, b, m, eng, banks=pt):
             if kind == "x":
-                bank = transposed(x_sb[b], m, banks)
+                bank = transposed_plain(xp[m], banks) if b in PERM_X else transposed(x_sb[b], m, banks)
                 nh = 1 if b < SPLIT else 2
                 dst = xg[b % 2][:].bitcast(F32).rearrange("p (h a c u) -> p h a c u", h=nh, a=6, u=2)
                 src = bank[:].rearrange("p (a u h c) -> p h a c u", a=2, u=2, h=nh)
@@ -245,9 +250,11 @@ def tile_bilinearpairedlayer_pb_t_kernel(tc, t_bil, x_r, W_r, b_r, b_bil, out):
                 nc.vector.tensor_tensor(out=dst, in0=bank[:].rearrange("p (k j) -> p j k", k=2),
                                         in1=bbt[:].rearrange("p (j k) -> p j k", k=2), op=ALU.add)
             o_view = out[b].rearrange("(p a) j k -> p a (j k)", a=4)
-            if b == LAST:
+            if b >= FINE:
                 nc.sync.dma_start(out=o_view[:, a, 512 * jh:512 * (jh + 1)], in_=row[:, 512 * jh:512 * (jh + 1)])
-            elif a % 2 == 1 and jh == 1:
+            elif b >= ROWS and jh == 1:
+                nc.sync.dma_start(out=o_view[:, a, :], in_=row)
+            elif b < ROWS and a % 2 == 1 and jh == 1:
                 o = o_sb[(2 * b + a // 2) % 4]
                 nc.sync.dma_start(out=o_view[:, a - 1:a + 1, :], in_=o[:].rearrange("p (a r) -> p a r", a=2))
 
@@ -282,7 +289,9 @@ def tile_bilinearpairedlayer_pb_t_kernel(tc, t_bil, x_r, W_r, b_r, b_bil, out):
             upto = nxt + sum(plans[tick + 1:tick + 1 + PERM_LEAD])
             for kind, b, m in jobs[cnt["perm"]:upto]:
                 if kind == "t" and m in PERM_M:
-                    permute(b, m)
+                    permute(t_sb[b % NT], tp[(4 * b + m) % 4], m, PERM_E[m])
+                if kind == "x" and b in PERM_X:
+                    permute(x_sb[b], xp[m], m, "v")
             cnt["perm"] = max(cnt["perm"], min(upto, len(jobs)))
 
         scores = [(b, a, jh) for b in range(SPLIT) for a in range(4) for jh in range(2)]
@@ -292,40 +301,46 @@ def tile_bilinearpairedlayer_pb_t_kernel(tc, t_bil, x_r, W_r, b_r, b_bil, out):
         for tick in range(4 * B):
             n = tick // 4
             q = tick % 4
-            for item in full1:
-                relu(item[0], item[1], item[2], item[3], item[4], item[5])
-            for item in full2:
-                leave(item[0], item[1], item[2], item[3])
-            full2 = []
-            for kind, b, m in jobs[nxt:nxt + plans[tick]]:
-                waiting += [(tick + QD[kind], item) for item in job(kind, b, m, "s")]
-            nxt += plans[tick]
-            full1 = s1(n, q)
-            if PERM_POS == "mid":
-                permute_ahead(tick)
-            if tick == BTICK:
-                spread_b_bil()
-            for b, a, jh in scores[0:S_CAP[0] if n < SPLIT else S_CAP[1] if n < LAST else S_CAP[2]]:
-                if ("h", b, jh) in ready and ("t", b, a // 2) in ready:
-                    full2.append(s2(b, a, jh, next_bank("p2", p2)))
-                else:
-                    break
-            scores = scores[len(full2):]
-            if tick >= 2 and q % 2 == 0:
-                b, h = (tick - 2) // 4, (tick - 2) % 4 // 2
-                if b >= SPLIT:
-                    regroup(b, 1024 * h, 1024, RG)
-                    qh(b, 1024 * h, 1024)
-                elif h == 1:
-                    regroup(b, 0, 2048, RG_ALL)
-                    qh(b, 0, 1024)
-                    qh(b, 1024, 1024)
-            for when, item in waiting:
-                if when <= tick or tick < 1:
-                    quantise(item[0], item[1], item[2])
-            waiting = [(when, item) for when, item in waiting if when > tick and tick >= 1]
-            if PERM_POS == "end":
-                permute_ahead(tick)
+            old1, old2 = full1, full2
+            full1, full2 = [], []
+            for what in ORDER:
+                if what == "U":
+                    for item in old1:
+                        relu(item[0], item[1], item[2], item[3], item[4], item[5])
+                elif what == "L":
+                    for item in old2:
+                        leave(item[0], item[1], item[2], item[3])
+                elif what == "F":
+                    for kind, b, m in jobs[nxt:nxt + plans[tick]]:
+                        waiting += [(tick + QD[kind], item) for item in job(kind, b, m, "s")]
+                    nxt += plans[tick]
+                elif what == "A":
+                    full1 = s1(n, q)
+                    if tick == BTICK:
+                        spread_b_bil()
+                elif what == "C":
+                    for b, a, jh in scores[0:S_CAP[0] if n < SPLIT else S_CAP[1] if n < LAST else S_CAP[2]]:
+                        if ("h", b, jh) in ready and ("t", b, a // 2) in ready:
+                            full2.append(s2(b, a, jh, next_bank("p2", p2)))
+                        else:
+                            break
+                    scores = scores[len(full2):]
+                elif what == "R" and tick >= 2 and q % 2 == 0:
+                    b, h = (tick - 2) // 4, (tick - 2) % 4 // 2
+                    if b >= SPLIT:
+                        regroup(b, 1024 * h, 1024, RG)
+                        qh(b, 1024 * h, 1024)
+                    elif h == 1:
+                        regroup(b, 0, 2048, RG_ALL)
+                        qh(b, 0, 1024)
+                        qh(b, 1024, 1024)
+                elif what == "Q":
+                    for when, item in waiting:
+                        if when <= tick or tick < 1:
+                            quantise(item[0], item[1], item[2])
+                    waiting = [(when, item) for when, item in waiting if when > tick and tick >= 1]
+                elif what == "P":
+                    permute_ahead(tick)
         for item in full1:
             relu(item[0], item[1], item[2], item[3], item[4], item[5])
         assert scores == [(LAST, a, 1) for a in range(4)] and len(full2) == 4

@@ -16,26 +16,8 @@ B = 8
 LAST = B - 1
 FLOPS = 2 * 8 * 512 * 512 * 1536 + 2 * 8 * 1024 * 512 * 512
 
-BANKS_T, BANKS_1, BANKS_2 = 2, 2, 4
-HEAD = "vsvsssss"
-BTICK = 2
-QD = {"x": 1, "t": 1, "w": 0}
-SLOTS = ((0, 2, 2, 2), (2, 2, 0, 2))
-RG = ("g", "v")
-RG_ALL = ("v", "g", "s")
-RG_END = ("v",)
-ON_S = ((5, 1, 0), (5, 3, 0), (6, 3, 0), (6, 3, 1), (7, 2, 0), (7, 2, 1))
-NT = 4
-PERM_M = ()
-FINE = 6
-ROWS = 6
-PERM_E = "ssss"
-PERM_X = ()
-PERM_LEAD = 2
-ORDER = "ULFACRQP"
-SPLIT = 6
-S_CAP = (2, 2, 4)
-EXTRA = ()
+HALVED = 6
+T_TILES = 4
 
 
 def tile_bilinearpairedlayer_pb_t_kernel(tc, t_bil, x_r, W_r, b_r, b_bil, out):
@@ -45,312 +27,281 @@ def tile_bilinearpairedlayer_pb_t_kernel(tc, t_bil, x_r, W_r, b_r, b_bil, out):
         ps = ctx.enter_context(tc.psum_pool(name="ps", bufs=1))
 
         ident = sb.tile([P, P], F32, name="ident")
-        x_sb = [sb.tile([P, 2048], BF16, name="x%d" % i) for i in range(B)]
-        t_sb = [sb.tile([P, 4096], BF16, name="t%d" % i) for i in range(NT)]
-        w_sb = sb.tile([P, 6144], BF16, name="w_sb")
-        wg = sb.tile([P, 6144], BF16, name="wg", align_bytes=64)
-        wc = sb.tile([P, 1536], U32, name="wc", align_bytes=64)
-        ws = sb.tile([P, 1536], U8, name="ws", align_bytes=64)
-        xg = [sb.tile([P, 3072], BF16, name="xg%d" % i, align_bytes=64) for i in range(2)]
-        xc = [sb.tile([P, 768], U32, name="xc%d" % i, align_bytes=64) for i in range(3)]
-        xs = [sb.tile([P, 768], U8, name="xs%d" % i, align_bytes=64) for i in range(3)]
-        tp = [sb.tile([P, 512], F32, name="tp%d" % i) for i in range(4)]
-        xp = [sb.tile([P, 512], F32, name="xp%d" % i) for i in range(2)]
-        tg = [sb.tile([P, 2048], BF16, name="tg%d" % i, align_bytes=64) for i in range(4)]
-        tcd = [sb.tile([P, 1024], U32, name="tcd%d" % i, align_bytes=64) for i in range(3)]
-        tsc = [sb.tile([P, 1024], U8, name="tsc%d" % i, align_bytes=64) for i in range(3)]
-        hrt = [sb.tile([P, 2048], BF16, name="hrt%d" % i) for i in range(2)]
-        hg = [sb.tile([P, 2048], BF16, name="hg%d" % i, align_bytes=64) for i in range(2)]
-        hc = [sb.tile([P, 512], U32, name="hc%d" % i, align_bytes=64) for i in range(3)]
-        hs = [sb.tile([P, 512], U8, name="hs%d" % i, align_bytes=64) for i in range(3)]
+        x_raw = [sb.tile([P, 2048], BF16, name="x_raw%d" % i) for i in range(B)]
+        t_raw = [sb.tile([P, 4096], BF16, name="t_raw%d" % i) for i in range(T_TILES)]
+        w_raw = sb.tile([P, 6144], BF16, name="w_raw")
+        w_four = sb.tile([P, 6144], BF16, name="w_four", align_bytes=256)
+        w_codes = sb.tile([P, 1536], U32, name="w_codes", align_bytes=256)
+        w_scales = sb.tile([P, 1536], U8, name="w_scales", align_bytes=256)
+        x_four = [sb.tile([P, 3072], BF16, name="x_four%d" % i, align_bytes=256) for i in range(2)]
+        x_codes = [sb.tile([P, 768], U32, name="x_codes%d" % i, align_bytes=256) for i in range(3)]
+        x_scales = [sb.tile([P, 768], U8, name="x_scales%d" % i, align_bytes=256) for i in range(3)]
+        t_four = [sb.tile([P, 2048], BF16, name="t_four%d" % i, align_bytes=256) for i in range(4)]
+        t_codes = [sb.tile([P, 1024], U32, name="t_codes%d" % i, align_bytes=256) for i in range(3)]
+        t_scales = [sb.tile([P, 1024], U8, name="t_scales%d" % i, align_bytes=256) for i in range(3)]
+        h_rows = [sb.tile([P, 2048], BF16, name="h_rows%d" % i) for i in range(2)]
+        h_four = [sb.tile([P, 2048], BF16, name="h_four%d" % i, align_bytes=256) for i in range(2)]
+        h_codes = [sb.tile([P, 512], U32, name="h_codes%d" % i, align_bytes=256) for i in range(3)]
+        h_scales = [sb.tile([P, 512], U8, name="h_scales%d" % i, align_bytes=256) for i in range(3)]
         o_sb = [sb.tile([P, 2048], F32, name="o%d" % i) for i in range(4)]
         br_bf = sb.tile([P, 4], BF16, name="br_bf")
-        rows = sb.tile([P, 2], BF16, name="rows")
-        ones = sb.tile([P, P], BF16, name="ones")
         br = sb.tile([P, 4], F32, name="br")
-        bbt = sb.tile([P, 512], F32, name="bbt")
-        bbf = sb.tile([P, 2], F32, name="bbf")
+        b_row = sb.tile([P, 2], BF16, name="b_row")
+        ones = sb.tile([P, P], BF16, name="ones")
+        bb = sb.tile([P, 2], F32, name="bb")
+        bb_pairs = sb.tile([P, 512], F32, name="bb_pairs")
 
-        pt = [ps.tile([P, 512], F32, name="pt%d" % i) for i in range(BANKS_T)]
-        p1 = [ps.tile([P, 512], F32, name="p1_%d" % i) for i in range(BANKS_1)]
-        p2 = [ps.tile([P, 512], F32, name="p2_%d" % i) for i in range(BANKS_2)]
-        cnt = {"pt": 0, "p1": 0, "p2": 0}
+        flip_banks = [ps.tile([P, 512], F32, name="flip%d" % i) for i in range(2)]
+        hidden_banks = [ps.tile([P, 512], F32, name="hidden%d" % i) for i in range(2)]
+        score_banks = [ps.tile([P, 512], F32, name="score%d" % i) for i in range(4)]
+        used = {"flip": 0, "hidden": 0, "score": 0}
+
+        def next_bank(kind, banks):
+            bank = banks[used[kind] % len(banks)]
+            used[kind] += 1
+            return bank
 
         ctx.enter_context(tc.manual_schedule())
 
         def load_x(b):
-            nc.sync.dma_start(out=x_sb[b][:], in_=x_r[b].rearrange("(p a) f -> p (a f)", a=4))
+            nc.sync.dma_start(out=x_raw[b][:], in_=x_r[b].rearrange("(p a) f -> p (a f)", a=4))
 
         def load_t(b):
-            nc.sync.dma_start(out=t_sb[b % NT][:], in_=t_bil[b].rearrange("(p a) k g -> p (a k g)", a=4))
+            nc.sync.dma_start(out=t_raw[b % T_TILES][:], in_=t_bil[b].rearrange("(p a) k g -> p (a k g)", a=4))
 
         load_x(0)
         w_view = W_r.rearrange("(p t) f -> p (t f)", t=4)
-        for m in range(3):
-            nc.sync.dma_start(out=w_sb[:, 2048 * m:2048 * (m + 1)], in_=w_view[:, 2048 * m:2048 * (m + 1)])
-        with nc.allow_non_contiguous_dma(reason="four bfloat16 of b_r to a partition"):
-            nc.scalar.dma_start(out=br_bf[:], in_=b_r.rearrange("(p t) -> p t", t=4))
-        nc.vector.memset(rows[:], 0.0)
-        nc.vector.memset(ones[:], 1.0)
-        nc.scalar.dma_start(out=rows[0:1, :], in_=b_bil.unsqueeze(0))
+        for third in range(3):
+            cols = slice(2048 * third, 2048 * (third + 1))
+            nc.sync.dma_start(out=w_raw[:, cols], in_=w_view[:, cols])
         load_t(0)
         load_x(1)
+        nc.vector.memset(b_row[:], 0.0)
+        nc.vector.memset(ones[:], 1.0)
+        with nc.allow_non_contiguous_dma(reason="four bfloat16 of b_r to a partition"):
+            nc.scalar.dma_start(out=br_bf[:], in_=b_r.rearrange("(p t) -> p t", t=4))
+        nc.scalar.dma_start(out=b_row[0:1, :], in_=b_bil.unsqueeze(0))
         for b in range(1, B):
             if b + 1 < B:
                 load_x(b + 1)
-            if b < NT:
+            if b < T_TILES:
                 load_t(b)
 
         masks.make_identity(nc, ident[:])
-        for i in range(2):
-            nc.vector.memset(xg[i][:, 0:4], 0.0)
-            nc.vector.memset(xg[i][:, 3068:3072], 0.0)
+        for four in x_four:
+            nc.vector.memset(four[:, 0:4], 0.0)
+            nc.vector.memset(four[:, 3068:3072], 0.0)
 
-        def next_bank(which, banks):
-            bank = banks[cnt[which] % len(banks)]
-            cnt[which] += 1
-            return bank
-
-        def copy_on(eng, o_ap, i_ap):
-            if eng == "v":
-                nc.vector.tensor_copy(out=o_ap, in_=i_ap)
-            elif eng == "s":
-                nc.scalar.copy(out=o_ap, in_=i_ap)
+        def copy_on(eng, out_ap, in_ap):
+            if eng == "vector":
+                nc.vector.tensor_copy(out=out_ap, in_=in_ap)
+            elif eng == "scalar":
+                nc.scalar.copy(out=out_ap, in_=in_ap)
             else:
-                nc.gpsimd.tensor_scalar(out=o_ap, in0=i_ap, scalar1=1.0, scalar2=0.0, op0=ALU.mult, op1=ALU.add)
+                nc.gpsimd.tensor_scalar(out=out_ap, in0=in_ap, scalar1=1.0, scalar2=0.0, op0=ALU.mult, op1=ALU.add)
 
-        def quant(codes, scales, c_off, src, s_off, width):
-            nc.vector.quantize_mx(out=codes[:, c_off:c_off + width // 4].bitcast(FP8X4),
-                                  scales=scales[:, c_off:c_off + width // 4],
-                                  in_=src[:, s_off:s_off + width])
+        def quantise(codes, scales, c_out, four, c_in, width):
+            nc.vector.quantize_mx(out=codes[:, c_out:c_out + width // 4].bitcast(FP8X4),
+                                  scales=scales[:, c_out:c_out + width // 4],
+                                  in_=four[:, c_in:c_in + width])
 
-        def permute(src, dst, m, eng):
-            copy_on(eng, dst[:].rearrange("p (r u w) -> p r u w", r=2, u=2),
-                    src[:].bitcast(F32)[:, 512 * m:512 * (m + 1)].rearrange("p (r w u) -> p r u w", r=2, u=2))
-
-        def transposed_plain(src, banks):
-            bank = next_bank("pt", banks)
-            for i in range(4):
-                nc.tensor.transpose(bank[:, 128 * i:128 * (i + 1)], src[:, 128 * i:128 * (i + 1)], ident[:])
-            return bank
-
-        def transposed(src, m, banks):
-            bank = next_bank("pt", banks)
+        def transpose_bank(raw, m, banks):
+            bank = next_bank("flip", banks)
+            words = raw[:].bitcast(F32)
             for i in range(4):
                 c0 = 512 * m + 256 * (i // 2)
-                nc.tensor.transpose(bank[:, 128 * i:128 * (i + 1)], src[:].bitcast(F32)[:, c0 + i % 2:c0 + 256:2], ident[:])
+                nc.tensor.transpose(bank[:, 128 * i:128 * (i + 1)], words[:, c0 + i % 2:c0 + 256:2], ident[:])
             return bank
 
-        def job(kind, b, m, eng, banks=pt):
+        def flip(kind, b, m, eng, banks):
             if kind == "x":
-                bank = transposed_plain(xp[m], banks) if b in PERM_X else transposed(x_sb[b], m, banks)
-                nh = 1 if b < SPLIT else 2
-                dst = xg[b % 2][:].bitcast(F32).rearrange("p (h a c u) -> p h a c u", h=nh, a=6, u=2)
-                src = bank[:].rearrange("p (a u h c) -> p h a c u", a=2, u=2, h=nh)
-                for h in range(nh):
+                bank = transpose_bank(x_raw[b], m, banks)
+                halves = 1 if b < HALVED else 2
+                dst = x_four[b % 2][:].bitcast(F32).rearrange("p (h a c u) -> p h a c u", h=halves, a=6, u=2)
+                src = bank[:].rearrange("p (a u h c) -> p h a c u", a=2, u=2, h=halves)
+                for h in range(halves):
                     copy_on(eng, dst[:, h, 1 + 2 * m:3 + 2 * m], src[:, h])
                 return [("x", b, 0)] if m == 1 else []
             if kind == "w":
-                src, dst, c0 = w_sb, wg, 512 * m
+                raw, four, c0 = w_raw, w_four, 512 * m
             else:
-                src, dst, c0 = t_sb[b % NT], tg[(2 * b + m // 2) % 4], 512 * (m % 2)
-            if kind == "t" and m in PERM_M:
-                bank = transposed_plain(tp[(4 * b + m) % 4], banks)
-            else:
-                bank = transposed(src, m, banks)
-            copy_on(eng, dst[:].bitcast(F32)[:, c0:c0 + 512].rearrange("p (a c u) -> p a c u", a=2, u=2),
+                raw, four, c0 = t_raw[b % T_TILES], t_four[(2 * b + m // 2) % 4], 512 * (m % 2)
+            bank = transpose_bank(raw, m, banks)
+            copy_on(eng, four[:].bitcast(F32)[:, c0:c0 + 512].rearrange("p (a c u) -> p a c u", a=2, u=2),
                     bank[:].rearrange("p (a u c) -> p a c u", a=2, u=2))
-            if kind == "t" and m == 3 and b + NT < B:
-                load_t(b + NT)
+            if kind == "t" and m == 3 and b + T_TILES < B:
+                load_t(b + T_TILES)
             return [(kind, b, m // 2)] if m % 2 == 1 else []
 
         ready = set()
 
-        def quantise(kind, b, h):
+        def make_operand(kind, b, h):
             ready.add((kind, b, h))
-            if kind == "x":
-                g = xg[b % 2]
-                if b < SPLIT:
-                    nc.vector.tensor_copy(out=g[:, 4:512], in_=g[:, 2048:2556])
-                    nc.vector.tensor_copy(out=g[:, 2560:3068], in_=g[:, 516:1024])
-                else:
-                    gh = g[:].rearrange("p (h c) -> p h c", h=2)
-                    nc.vector.tensor_copy(out=gh[:, :, 4:256], in_=gh[:, :, 1024:1276])
-                    nc.vector.tensor_copy(out=gh[:, :, 1280:1532], in_=gh[:, :, 260:512])
-                    nc.vector.tensor_copy(out=g[:, 1536:1540], in_=g[:, 1276:1280])
-                    nc.vector.tensor_copy(out=g[:, 1532:1536], in_=g[:, 1792:1796])
-                quant(xc[b % 3], xs[b % 3], 0, g, 0, 2048)
-                quant(xc[b % 3], xs[b % 3], 512, g, 2048, 1024)
-            elif kind == "w":
-                quant(wc, ws, 512 * h, wg, 2048 * h, 2048)
+            if kind == "w":
+                quantise(w_codes, w_scales, 512 * h, w_four, 2048 * h, 2048)
+            elif kind == "t":
+                quantise(t_codes[b % 3], t_scales[b % 3], 512 * h, t_four[(2 * b + h) % 4], 0, 2048)
             else:
-                quant(tcd[b % 3], tsc[b % 3], 512 * h, tg[(2 * b + h) % 4], 0, 2048)
+                four = x_four[b % 2]
+                if b < HALVED:
+                    nc.vector.tensor_copy(out=four[:, 4:512], in_=four[:, 2048:2556])
+                    nc.vector.tensor_copy(out=four[:, 2560:3068], in_=four[:, 516:1024])
+                else:
+                    half = four[:].rearrange("p (h c) -> p h c", h=2)
+                    nc.vector.tensor_copy(out=half[:, :, 4:256], in_=half[:, :, 1024:1276])
+                    nc.vector.tensor_copy(out=half[:, :, 1280:1532], in_=half[:, :, 260:512])
+                    nc.vector.tensor_copy(out=four[:, 1536:1540], in_=four[:, 1276:1280])
+                    nc.vector.tensor_copy(out=four[:, 1532:1536], in_=four[:, 1792:1796])
+                quantise(x_codes[b % 3], x_scales[b % 3], 0, four, 0, 2048)
+                quantise(x_codes[b % 3], x_scales[b % 3], 512, four, 2048, 1024)
 
-        def hidden(t, bank, c_bank, codes, scales, c_x, width):
-            step = width // 4
-            for w, off in ((2, 0), (0, step), (1, 2 * step)):
-                s = t * 3 + w
+        def hidden_group(b, t, bank, c_bank, c_x, width):
+            block = width // 4
+            for w, shift in ((2, 0), (0, 1), (1, 2)):
+                ws = slice((3 * t + w) * 128, (3 * t + w + 1) * 128)
+                xs = slice(c_x + shift * block, c_x + shift * block + width)
                 nc.tensor.matmul_mx(out=bank[:, c_bank:c_bank + width],
-                                    lhsT=wc[:, s * 128:(s + 1) * 128].bitcast(FP8X4),
-                                    lhsT_scale=ws[:, s * 128:(s + 1) * 128],
-                                    rhs=codes[:, c_x + off:c_x + off + width].bitcast(FP8X4),
-                                    rhs_scale=scales[:, c_x + off:c_x + off + width],
-                                    start=(w == 2), stop=(w == 1))
+                                    lhsT=w_codes[:, ws].bitcast(FP8X4), lhsT_scale=w_scales[:, ws],
+                                    rhs=x_codes[b % 3][:, xs].bitcast(FP8X4), rhs_scale=x_scales[b % 3][:, xs],
+                                    start=(shift == 0), stop=(shift == 2))
+
+        def hidden(b, q):
+            bank = next_bank("hidden", hidden_banks)
+            if b < HALVED:
+                hidden_group(b, q, bank, 0, 0, 512)
+                return [(b, q, bank, 0, 512 * q, 512)]
+            h = q // 2
+            relus = []
+            for i in range(2):
+                t = 2 * (q % 2) + i
+                hidden_group(b, t, bank, 256 * i, 384 * h, 256)
+                relus.append((b, t, bank, 256 * i, 1024 * h + 256 * t, 256))
+            return relus
 
         def relu(b, t, bank, c_bank, c_out, width):
-            nc.scalar.activation(out=hrt[b % 2][:, c_out:c_out + width].rearrange("p (q a) -> p q a", a=4),
+            nc.scalar.activation(out=h_rows[b % 2][:, c_out:c_out + width].rearrange("p (q a) -> p q a", a=4),
                                  in_=bank[:, c_bank:c_bank + width].rearrange("p (a q) -> p q a", a=4),
                                  func=ACT.Relu, bias=br[:, t:t + 1], scale=1.0)
 
-        def s1(b, q):
-            bank = next_bank("p1", p1)
-            if b < SPLIT:
-                hidden(q, bank, 0, xc[b % 3], xs[b % 3], 0, 512)
-                return [(b, q, bank, 0, 512 * q, 512)]
-            h = q // 2
-            done = []
-            for i in range(2):
-                t = 2 * (q % 2) + i
-                hidden(t, bank, 256 * i, xc[b % 3], xs[b % 3], 384 * h, 256)
-                done.append((b, t, bank, 256 * i, 1024 * h + 256 * t, 256))
-            return done
+        def regroup(b, c0, width, engines):
+            dst = h_four[b % 2][:, c0:c0 + width].rearrange("p (j t) -> p j t", t=4)
+            src = h_rows[b % 2][:, c0:c0 + width].rearrange("p (t j) -> p j t", t=4)
+            runs = width // 64
+            for i in range(len(engines)):
+                share = slice(runs * i // len(engines) * 16, runs * (i + 1) // len(engines) * 16)
+                copy_on(engines[i], dst[:, share], src[:, share])
 
-        def regroup(b, off, width, engines):
-            n = len(engines)
-            dst = hg[b % 2][:, off:off + width].rearrange("p (c t) -> p c t", t=4)
-            src = hrt[b % 2][:, off:off + width].rearrange("p (t c) -> p c t", t=4)
-            blocks = width // 64
-            for i in range(n):
-                c0, c1 = blocks * i // n * 16, blocks * (i + 1) // n * 16
-                copy_on(engines[i], dst[:, c0:c1], src[:, c0:c1])
+        def quantise_hidden(b, h):
+            quantise(h_codes[b % 3], h_scales[b % 3], 256 * h, h_four[b % 2], 1024 * h, 1024)
+            ready.add(("h", b, h))
 
-        def qh(b, off, width):
-            quant(hc[b % 3], hs[b % 3], off // 4, hg[b % 2], off, width)
-            ready.add(("h", b, off // 1024))
+        def score(b, a, k, h, bank):
+            ts = slice((2 * a + k) * 128, (2 * a + k + 1) * 128)
+            hs = slice(256 * h, 256 * (h + 1))
+            nc.tensor.matmul_mx(out=bank[:, 256 * k:256 * (k + 1)],
+                                lhsT=t_codes[b % 3][:, ts].bitcast(FP8X4), lhsT_scale=t_scales[b % 3][:, ts],
+                                rhs=h_codes[b % 3][:, hs].bitcast(FP8X4), rhs_scale=h_scales[b % 3][:, hs],
+                                start=True, stop=True)
 
-        def s2(b, a, jh, bank):
+        def scores(b, a, halves, banks):
             for k in range(2):
-                s = 2 * a + k
-                nc.tensor.matmul_mx(out=bank[:, k * 256:(k + 1) * 256],
-                                    lhsT=tcd[b % 3][:, s * 128:(s + 1) * 128].bitcast(FP8X4),
-                                    lhsT_scale=tsc[b % 3][:, s * 128:(s + 1) * 128],
-                                    rhs=hc[b % 3][:, jh * 256:(jh + 1) * 256].bitcast(FP8X4),
-                                    rhs_scale=hs[b % 3][:, jh * 256:(jh + 1) * 256],
-                                    start=True, stop=True)
-            return (b, a, jh, bank)
+                for h, bank in zip(halves, banks):
+                    score(b, a, k, h, bank)
+            return [(b, a, h, bank) for h, bank in zip(halves, banks)]
 
-        def leave(b, a, jh, bank):
+        def leave(b, a, h, bank):
             row = o_sb[(2 * b + a // 2) % 4][:, 1024 * (a % 2):1024 * (a % 2 + 1)]
-            dst = row[:, 512 * jh:512 * (jh + 1)].rearrange("p (j k) -> p j k", k=2)
-            if (b, a, jh) in ON_S:
+            dst = row[:, 512 * h:512 * (h + 1)].rearrange("p (j k) -> p j k", k=2)
+            if (b, a) in ((LAST - 1, 3), (LAST, 2)):
                 for k in range(2):
-                    nc.scalar.activation(out=dst[:, :, k], in_=bank[:, k * 256:(k + 1) * 256],
-                                         func=ACT.Identity, bias=bbf[:, k:k + 1], scale=1.0)
+                    nc.scalar.activation(out=dst[:, :, k], in_=bank[:, 256 * k:256 * (k + 1)],
+                                         func=ACT.Identity, bias=bb[:, k:k + 1], scale=1.0)
             else:
                 nc.vector.tensor_tensor(out=dst, in0=bank[:].rearrange("p (k j) -> p j k", k=2),
-                                        in1=bbt[:].rearrange("p (j k) -> p j k", k=2), op=ALU.add)
+                                        in1=bb_pairs[:].rearrange("p (j k) -> p j k", k=2), op=ALU.add)
             o_view = out[b].rearrange("(p a) j k -> p a (j k)", a=4)
-            if b >= FINE:
-                nc.sync.dma_start(out=o_view[:, a, 512 * jh:512 * (jh + 1)], in_=row[:, 512 * jh:512 * (jh + 1)])
-            elif b >= ROWS and jh == 1:
+            if b >= HALVED:
+                nc.sync.dma_start(out=o_view[:, a, 512 * h:512 * (h + 1)], in_=row[:, 512 * h:512 * (h + 1)])
+            elif h == 1:
                 nc.sync.dma_start(out=o_view[:, a, :], in_=row)
-            elif b < ROWS and a % 2 == 1 and jh == 1:
-                o = o_sb[(2 * b + a // 2) % 4]
-                nc.sync.dma_start(out=o_view[:, a - 1:a + 1, :], in_=o[:].rearrange("p (a r) -> p a r", a=2))
 
         def spread_b_bil():
-            bank = next_bank("p2", p2)
-            nc.tensor.matmul(out=bank[:, 0:2], lhsT=ones[:], rhs=rows[:], start=True, stop=True)
-            nc.vector.tensor_copy(out=bbf[:], in_=bank[:, 0:2])
-            nc.vector.tensor_copy(out=bbt[:].rearrange("p (j k) -> p j k", k=2),
-                                  in_=bbf[:].unsqueeze(1).to_broadcast([P, 256, 2]))
+            bank = next_bank("score", score_banks)
+            nc.tensor.matmul(out=bank[:, 0:2], lhsT=ones[:], rhs=b_row[:], start=True, stop=True)
+            nc.vector.tensor_copy(out=bb[:], in_=bank[:, 0:2])
+            nc.vector.tensor_copy(out=bb_pairs[:].rearrange("p (j k) -> p j k", k=2),
+                                  in_=bb[:].unsqueeze(1).to_broadcast([P, 256, 2]))
 
-        jobs = [("x", 0, 0), ("x", 0, 1)] + [("w", 0, m) for m in range(6)]
-        head = 8
-        for b in range(B):
-            jobs += [("t", b, 0), ("t", b, 1)]
-            if b < LAST:
-                jobs += [("x", b + 1, 0), ("x", b + 1, 1)]
-            jobs += [("t", b, 2), ("t", b, 3)]
-        todo = []
-        for i in range(head):
-            todo += job(jobs[i][0], jobs[i][1], jobs[i][2], HEAD[i], pt + p2)
-            if i in (3, 5):
-                for item in todo:
-                    quantise(item[0], item[1], item[2])
-                todo = []
-        waiting = [(0, item) for item in todo]
+        to_make = []
+        head = [("x", 0, 0), ("x", 0, 1)] + [("w", 0, m) for m in range(6)]
+        for i in range(len(head)):
+            kind, b, m = head[i]
+            to_make += flip(kind, b, m, "vector" if m == 0 else "scalar", flip_banks + score_banks)
+            if kind == "w" and m in (1, 3):
+                for item in to_make:
+                    make_operand(item[0], item[1], item[2])
+                to_make = []
+        waiting = [(0, item) for item in to_make]
         nc.vector.tensor_copy(out=br[:], in_=br_bf[:])
-        nxt = head
-        plans = [2 if tick in EXTRA else SLOTS[min(tick // 4, 1)][tick % 4] for tick in range(4 * B)] + [0]
-        cnt["perm"] = head
 
-        def permute_ahead(tick):
-            upto = nxt + sum(plans[tick + 1:tick + 1 + PERM_LEAD])
-            for kind, b, m in jobs[cnt["perm"]:upto]:
-                if kind == "t" and m in PERM_M:
-                    permute(t_sb[b % NT], tp[(4 * b + m) % 4], m, PERM_E[m])
-                if kind == "x" and b in PERM_X:
-                    permute(x_sb[b], xp[m], m, "v")
-            cnt["perm"] = max(cnt["perm"], min(upto, len(jobs)))
-
-        scores = [(b, a, jh) for b in range(SPLIT) for a in range(4) for jh in range(2)]
-        scores += [(b, a, jh) for b in range(SPLIT, B) for jh in range(2) for a in range(4)]
-        full1 = []
-        full2 = []
+        flips = []
+        for b in range(B):
+            flips += [("t", b, 0), ("t", b, 1)]
+            if b < LAST:
+                flips += [("x", b + 1, 0), ("x", b + 1, 1)]
+            flips += [("t", b, 2), ("t", b, 3)]
+        rows = [(b, a, (0, 1)) for b in range(HALVED) for a in range(4)]
+        rows += [(b, a, (h,)) for b in range(HALVED, B) for h in range(2) for a in range(4)]
+        relus, full = [], []
         for tick in range(4 * B):
             n = tick // 4
             q = tick % 4
-            old1, old2 = full1, full2
-            full1, full2 = [], []
-            for what in ORDER:
-                if what == "U":
-                    for item in old1:
-                        relu(item[0], item[1], item[2], item[3], item[4], item[5])
-                elif what == "L":
-                    for item in old2:
-                        leave(item[0], item[1], item[2], item[3])
-                elif what == "F":
-                    for kind, b, m in jobs[nxt:nxt + plans[tick]]:
-                        waiting += [(tick + QD[kind], item) for item in job(kind, b, m, "s")]
-                    nxt += plans[tick]
-                elif what == "A":
-                    full1 = s1(n, q)
-                    if tick == BTICK:
-                        spread_b_bil()
-                elif what == "C":
-                    for b, a, jh in scores[0:S_CAP[0] if n < SPLIT else S_CAP[1] if n < LAST else S_CAP[2]]:
-                        if ("h", b, jh) in ready and ("t", b, a // 2) in ready:
-                            full2.append(s2(b, a, jh, next_bank("p2", p2)))
-                        else:
-                            break
-                    scores = scores[len(full2):]
-                elif what == "R" and tick >= 2 and q % 2 == 0:
-                    b, h = (tick - 2) // 4, (tick - 2) % 4 // 2
-                    if b >= SPLIT:
-                        regroup(b, 1024 * h, 1024, RG)
-                        qh(b, 1024 * h, 1024)
-                    elif h == 1:
-                        regroup(b, 0, 2048, RG_ALL)
-                        qh(b, 0, 1024)
-                        qh(b, 1024, 1024)
-                elif what == "Q":
-                    for when, item in waiting:
-                        if when <= tick or tick < 1:
-                            quantise(item[0], item[1], item[2])
-                    waiting = [(when, item) for when, item in waiting if when > tick and tick >= 1]
-                elif what == "P":
-                    permute_ahead(tick)
-        for item in full1:
-            relu(item[0], item[1], item[2], item[3], item[4], item[5])
-        assert scores == [(LAST, a, 1) for a in range(4)] and len(full2) == 4
-        for item in full2[0:3:2]:
-            leave(item[0], item[1], item[2], item[3])
-        regroup(LAST, 1024, 1024, RG_END)
-        qh(LAST, 1024, 1024)
-        for item in full2[1:4:2]:
-            leave(item[0], item[1], item[2], item[3])
-        banks = [p1[0], pt[0], pt[1], p2[0]]
-        full2 = [s2(LAST, a, 1, banks[a]) for a in range(4)]
-        for item in full2:
-            leave(item[0], item[1], item[2], item[3])
+            for b, t, bank, c_bank, c_out, width in relus:
+                relu(b, t, bank, c_bank, c_out, width)
+            for b, a, h, bank in full:
+                leave(b, a, h, bank)
+
+            if q != (0 if n == 0 else 2):
+                for kind, b, m in flips[0:2]:
+                    waiting += [(tick + 1, item) for item in flip(kind, b, m, "scalar", flip_banks)]
+                flips = flips[2:]
+            relus = hidden(n, q)
+            if tick == 2:
+                spread_b_bil()
+
+            full = []
+            most = 4 if n == LAST else 2
+            while rows and len(full) + len(rows[0][2]) <= most:
+                b, a, halves = rows[0]
+                if ("h", b, halves[-1]) not in ready or ("t", b, a // 2) not in ready:
+                    break
+                full += scores(b, a, halves, [next_bank("score", score_banks) for h in halves])
+                rows = rows[1:]
+
+            if q == 0 and 1 <= n <= HALVED:
+                regroup(n - 1, 0, 2048, ("vector", "gpsimd", "scalar"))
+                quantise_hidden(n - 1, 0)
+                quantise_hidden(n - 1, 1)
+            elif q % 2 == 0 and tick >= 4 * HALVED + 2:
+                b, h = (tick - 2) // 4, (tick - 2) % 4 // 2
+                regroup(b, 1024 * h, 1024, ("gpsimd", "vector"))
+                quantise_hidden(b, h)
+            for when, item in waiting:
+                if when <= tick:
+                    make_operand(item[0], item[1], item[2])
+            waiting = [(when, item) for when, item in waiting if when > tick]
+
+        for b, t, bank, c_bank, c_out, width in relus:
+            relu(b, t, bank, c_bank, c_out, width)
+        for b, a, h, bank in full[0:3:2]:
+            leave(b, a, h, bank)
+        regroup(LAST, 1024, 1024, ("vector",))
+        quantise_hidden(LAST, 1)
+        for b, a, h, bank in full[1:4:2]:
+            leave(b, a, h, bank)
+        free = [hidden_banks[0], flip_banks[0], flip_banks[1], score_banks[0]]
+        full = []
+        for a in range(4):
+            full += scores(LAST, a, (1,), [free[a]])
+        for b, a, h, bank in full:
+            leave(b, a, h, bank)

from contextlib import ExitStack

import concourse.masks as masks
import concourse.mybir as mybir

F32 = mybir.dt.float32
BF16 = mybir.dt.bfloat16
U32 = mybir.dt.uint32
U8 = mybir.dt.uint8
FP8X4 = mybir.dt.float8_e4m3fn_x4
ACT = mybir.ActivationFunctionType
ALU = mybir.AluOpType

P = 128
B = 8
LAST = B - 1
FLOPS = 2 * 8 * 512 * 512 * 1536 + 2 * 8 * 1024 * 512 * 512

HALVED = 6
T_TILES = 4


def tile_bilinearpairedlayer_pb_t_kernel(tc, t_bil, x_r, W_r, b_r, b_bil, out):
    nc = tc.nc
    with ExitStack() as ctx:
        sb = ctx.enter_context(tc.tile_pool(name="sb", bufs=1))
        ps = ctx.enter_context(tc.psum_pool(name="ps", bufs=1))

        ident = sb.tile([P, P], F32, name="ident")
        x_raw = [sb.tile([P, 2048], BF16, name="x_raw%d" % i) for i in range(B)]
        t_raw = [sb.tile([P, 4096], BF16, name="t_raw%d" % i) for i in range(T_TILES)]
        w_raw = sb.tile([P, 6144], BF16, name="w_raw")
        w_four = sb.tile([P, 6144], BF16, name="w_four", align_bytes=256)
        w_codes = sb.tile([P, 1536], U32, name="w_codes", align_bytes=256)
        w_scales = sb.tile([P, 1536], U8, name="w_scales", align_bytes=256)
        x_four = [sb.tile([P, 3072], BF16, name="x_four%d" % i, align_bytes=256) for i in range(2)]
        x_codes = [sb.tile([P, 768], U32, name="x_codes%d" % i, align_bytes=256) for i in range(3)]
        x_scales = [sb.tile([P, 768], U8, name="x_scales%d" % i, align_bytes=256) for i in range(3)]
        t_four = [sb.tile([P, 2048], BF16, name="t_four%d" % i, align_bytes=256) for i in range(4)]
        t_codes = [sb.tile([P, 1024], U32, name="t_codes%d" % i, align_bytes=256) for i in range(3)]
        t_scales = [sb.tile([P, 1024], U8, name="t_scales%d" % i, align_bytes=256) for i in range(3)]
        h_rows = [sb.tile([P, 2048], BF16, name="h_rows%d" % i) for i in range(2)]
        h_four = [sb.tile([P, 2048], BF16, name="h_four%d" % i, align_bytes=256) for i in range(2)]
        h_codes = [sb.tile([P, 512], U32, name="h_codes%d" % i, align_bytes=256) for i in range(3)]
        h_scales = [sb.tile([P, 512], U8, name="h_scales%d" % i, align_bytes=256) for i in range(3)]
        o_sb = [sb.tile([P, 2048], F32, name="o%d" % i) for i in range(4)]
        br_bf = sb.tile([P, 4], BF16, name="br_bf")
        br = sb.tile([P, 4], F32, name="br")
        b_row = sb.tile([P, 2], BF16, name="b_row")
        ones = sb.tile([P, P], BF16, name="ones")
        bb = sb.tile([P, 2], F32, name="bb")
        bb_pairs = sb.tile([P, 512], F32, name="bb_pairs")

        flip_banks = [ps.tile([P, 512], F32, name="flip%d" % i) for i in range(2)]
        hidden_banks = [ps.tile([P, 512], F32, name="hidden%d" % i) for i in range(2)]
        score_banks = [ps.tile([P, 512], F32, name="score%d" % i) for i in range(4)]
        used = {"flip": 0, "hidden": 0, "score": 0}

        def next_bank(kind, banks):
            bank = banks[used[kind] % len(banks)]
            used[kind] += 1
            return bank

        ctx.enter_context(tc.manual_schedule())

        def load_x(b):
            nc.sync.dma_start(out=x_raw[b][:], in_=x_r[b].rearrange("(p a) f -> p (a f)", a=4))

        def load_t(b):
            nc.sync.dma_start(out=t_raw[b % T_TILES][:], in_=t_bil[b].rearrange("(p a) k g -> p (a k g)", a=4))

        load_x(0)
        w_view = W_r.rearrange("(p t) f -> p (t f)", t=4)
        for third in range(3):
            cols = slice(2048 * third, 2048 * (third + 1))
            nc.sync.dma_start(out=w_raw[:, cols], in_=w_view[:, cols])
        load_t(0)
        load_x(1)
        nc.vector.memset(b_row[:], 0.0)
        nc.vector.memset(ones[:], 1.0)
        with nc.allow_non_contiguous_dma(reason="four bfloat16 of b_r to a partition"):
            nc.scalar.dma_start(out=br_bf[:], in_=b_r.rearrange("(p t) -> p t", t=4))
        nc.scalar.dma_start(out=b_row[0:1, :], in_=b_bil.unsqueeze(0))
        for b in range(1, B):
            if b + 1 < B:
                load_x(b + 1)
            if b < T_TILES:
                load_t(b)

        masks.make_identity(nc, ident[:])
        for four in x_four:
            nc.vector.memset(four[:, 0:4], 0.0)
            nc.vector.memset(four[:, 3068:3072], 0.0)

        def copy_on(eng, out_ap, in_ap):
            if eng == "vector":
                nc.vector.tensor_copy(out=out_ap, in_=in_ap)
            elif eng == "scalar":
                nc.scalar.copy(out=out_ap, in_=in_ap)
            else:
                nc.gpsimd.tensor_scalar(out=out_ap, in0=in_ap, scalar1=1.0, scalar2=0.0, op0=ALU.mult, op1=ALU.add)

        def quantise(codes, scales, c_out, four, c_in, width):
            nc.vector.quantize_mx(out=codes[:, c_out:c_out + width // 4].bitcast(FP8X4),
                                  scales=scales[:, c_out:c_out + width // 4],
                                  in_=four[:, c_in:c_in + width])

        def transpose_bank(raw, m, banks):
            bank = next_bank("flip", banks)
            words = raw[:].bitcast(F32)
            for i in range(4):
                c0 = 512 * m + 256 * (i // 2)
                nc.tensor.transpose(bank[:, 128 * i:128 * (i + 1)], words[:, c0 + i % 2:c0 + 256:2], ident[:])
            return bank

        def flip(kind, b, m, eng, banks):
            if kind == "x":
                bank = transpose_bank(x_raw[b], m, banks)
                halves = 1 if b < HALVED else 2
                dst = x_four[b % 2][:].bitcast(F32).rearrange("p (h a c u) -> p h a c u", h=halves, a=6, u=2)
                src = bank[:].rearrange("p (a u h c) -> p h a c u", a=2, u=2, h=halves)
                for h in range(halves):
                    copy_on(eng, dst[:, h, 1 + 2 * m:3 + 2 * m], src[:, h])
                return [("x", b, 0)] if m == 1 else []
            if kind == "w":
                raw, four, c0 = w_raw, w_four, 512 * m
            else:
                raw, four, c0 = t_raw[b % T_TILES], t_four[(2 * b + m // 2) % 4], 512 * (m % 2)
            bank = transpose_bank(raw, m, banks)
            copy_on(eng, four[:].bitcast(F32)[:, c0:c0 + 512].rearrange("p (a c u) -> p a c u", a=2, u=2),
                    bank[:].rearrange("p (a u c) -> p a c u", a=2, u=2))
            if kind == "t" and m == 3 and b + T_TILES < B:
                load_t(b + T_TILES)
            return [(kind, b, m // 2)] if m % 2 == 1 else []

        ready = set()

        def make_operand(kind, b, h):
            ready.add((kind, b, h))
            if kind == "w":
                quantise(w_codes, w_scales, 512 * h, w_four, 2048 * h, 2048)
            elif kind == "t":
                quantise(t_codes[b % 3], t_scales[b % 3], 512 * h, t_four[(2 * b + h) % 4], 0, 2048)
            else:
                four = x_four[b % 2]
                if b < HALVED:
                    nc.vector.tensor_copy(out=four[:, 4:512], in_=four[:, 2048:2556])
                    nc.vector.tensor_copy(out=four[:, 2560:3068], in_=four[:, 516:1024])
                else:
                    half = four[:].rearrange("p (h c) -> p h c", h=2)
                    nc.vector.tensor_copy(out=half[:, :, 4:256], in_=half[:, :, 1024:1276])
                    nc.vector.tensor_copy(out=half[:, :, 1280:1532], in_=half[:, :, 260:512])
                    nc.vector.tensor_copy(out=four[:, 1536:1540], in_=four[:, 1276:1280])
                    nc.vector.tensor_copy(out=four[:, 1532:1536], in_=four[:, 1792:1796])
                quantise(x_codes[b % 3], x_scales[b % 3], 0, four, 0, 2048)
                quantise(x_codes[b % 3], x_scales[b % 3], 512, four, 2048, 1024)

        def hidden_group(b, t, bank, c_bank, c_x, width):
            block = width // 4
            for w, shift in ((2, 0), (0, 1), (1, 2)):
                ws = slice((3 * t + w) * 128, (3 * t + w + 1) * 128)
                xs = slice(c_x + shift * block, c_x + shift * block + width)
                nc.tensor.matmul_mx(out=bank[:, c_bank:c_bank + width],
                                    lhsT=w_codes[:, ws].bitcast(FP8X4), lhsT_scale=w_scales[:, ws],
                                    rhs=x_codes[b % 3][:, xs].bitcast(FP8X4), rhs_scale=x_scales[b % 3][:, xs],
                                    start=(shift == 0), stop=(shift == 2))

        def hidden(b, q):
            bank = next_bank("hidden", hidden_banks)
            if b < HALVED:
                hidden_group(b, q, bank, 0, 0, 512)
                return [(b, q, bank, 0, 512 * q, 512)]
            h = q // 2
            relus = []
            for i in range(2):
                t = 2 * (q % 2) + i
                hidden_group(b, t, bank, 256 * i, 384 * h, 256)
                relus.append((b, t, bank, 256 * i, 1024 * h + 256 * t, 256))
            return relus

        def relu(b, t, bank, c_bank, c_out, width):
            nc.scalar.activation(out=h_rows[b % 2][:, c_out:c_out + width].rearrange("p (q a) -> p q a", a=4),
                                 in_=bank[:, c_bank:c_bank + width].rearrange("p (a q) -> p q a", a=4),
                                 func=ACT.Relu, bias=br[:, t:t + 1], scale=1.0)

        def regroup(b, c0, width, engines):
            dst = h_four[b % 2][:, c0:c0 + width].rearrange("p (j t) -> p j t", t=4)
            src = h_rows[b % 2][:, c0:c0 + width].rearrange("p (t j) -> p j t", t=4)
            runs = width // 64
            for i in range(len(engines)):
                share = slice(runs * i // len(engines) * 16, runs * (i + 1) // len(engines) * 16)
                copy_on(engines[i], dst[:, share], src[:, share])

        def quantise_hidden(b, h):
            quantise(h_codes[b % 3], h_scales[b % 3], 256 * h, h_four[b % 2], 1024 * h, 1024)
            ready.add(("h", b, h))

        def score(b, a, k, h, bank):
            ts = slice((2 * a + k) * 128, (2 * a + k + 1) * 128)
            hs = slice(256 * h, 256 * (h + 1))
            nc.tensor.matmul_mx(out=bank[:, 256 * k:256 * (k + 1)],
                                lhsT=t_codes[b % 3][:, ts].bitcast(FP8X4), lhsT_scale=t_scales[b % 3][:, ts],
                                rhs=h_codes[b % 3][:, hs].bitcast(FP8X4), rhs_scale=h_scales[b % 3][:, hs],
                                start=True, stop=True)

        def scores(b, a, halves, banks):
            for k in range(2):
                for h, bank in zip(halves, banks):
                    score(b, a, k, h, bank)
            return [(b, a, h, bank) for h, bank in zip(halves, banks)]

        def leave(b, a, h, bank):
            row = o_sb[(2 * b + a // 2) % 4][:, 1024 * (a % 2):1024 * (a % 2 + 1)]
            dst = row[:, 512 * h:512 * (h + 1)].rearrange("p (j k) -> p j k", k=2)
            if (b, a) in ((LAST - 1, 3), (LAST, 2)):
                for k in range(2):
                    nc.scalar.activation(out=dst[:, :, k], in_=bank[:, 256 * k:256 * (k + 1)],
                                         func=ACT.Identity, bias=bb[:, k:k + 1], scale=1.0)
            else:
                nc.vector.tensor_tensor(out=dst, in0=bank[:].rearrange("p (k j) -> p j k", k=2),
                                        in1=bb_pairs[:].rearrange("p (j k) -> p j k", k=2), op=ALU.add)
            o_view = out[b].rearrange("(p a) j k -> p a (j k)", a=4)
            if b >= HALVED:
                nc.sync.dma_start(out=o_view[:, a, 512 * h:512 * (h + 1)], in_=row[:, 512 * h:512 * (h + 1)])
            elif h == 1:
                nc.sync.dma_start(out=o_view[:, a, :], in_=row)

        def spread_b_bil():
            bank = next_bank("score", score_banks)
            nc.tensor.matmul(out=bank[:, 0:2], lhsT=ones[:], rhs=b_row[:], start=True, stop=True)
            nc.vector.tensor_copy(out=bb[:], in_=bank[:, 0:2])
            nc.vector.tensor_copy(out=bb_pairs[:].rearrange("p (j k) -> p j k", k=2),
                                  in_=bb[:].unsqueeze(1).to_broadcast([P, 256, 2]))

        to_make = []
        head = [("x", 0, 0), ("x", 0, 1)] + [("w", 0, m) for m in range(6)]
        for i in range(len(head)):
            kind, b, m = head[i]
            to_make += flip(kind, b, m, "vector" if m == 0 else "scalar", flip_banks + score_banks)
            if kind == "w" and m in (1, 3):
                for item in to_make:
                    make_operand(item[0], item[1], item[2])
                to_make = []
        waiting = [(0, item) for item in to_make]
        nc.vector.tensor_copy(out=br[:], in_=br_bf[:])

        flips = []
        for b in range(B):
            flips += [("t", b, 0), ("t", b, 1)]
            if b < LAST:
                flips += [("x", b + 1, 0), ("x", b + 1, 1)]
            flips += [("t", b, 2), ("t", b, 3)]
        rows = [(b, a, (0, 1)) for b in range(HALVED) for a in range(4)]
        rows += [(b, a, (h,)) for b in range(HALVED, B) for h in range(2) for a in range(4)]
        relus, full = [], []
        for tick in range(4 * B):
            n = tick // 4
            q = tick % 4
            for b, t, bank, c_bank, c_out, width in relus:
                relu(b, t, bank, c_bank, c_out, width)
            for b, a, h, bank in full:
                leave(b, a, h, bank)

            if q != (0 if n == 0 else 2):
                for kind, b, m in flips[0:2]:
                    waiting += [(tick + 1, item) for item in flip(kind, b, m, "scalar", flip_banks)]
                flips = flips[2:]
            relus = hidden(n, q)
            if tick == 2:
                spread_b_bil()

            full = []
            most = 4 if n == LAST else 2
            while rows and len(full) + len(rows[0][2]) <= most:
                b, a, halves = rows[0]
                if ("h", b, halves[-1]) not in ready or ("t", b, a // 2) not in ready:
                    break
                full += scores(b, a, halves, [next_bank("score", score_banks) for h in halves])
                rows = rows[1:]

            if q == 0 and 1 <= n <= HALVED:
                regroup(n - 1, 0, 2048, ("vector", "gpsimd", "scalar"))
                quantise_hidden(n - 1, 0)
                quantise_hidden(n - 1, 1)
            elif q % 2 == 0 and tick >= 4 * HALVED + 2:
                b, h = (tick - 2) // 4, (tick - 2) % 4 // 2
                regroup(b, 1024 * h, 1024, ("gpsimd", "vector"))
                quantise_hidden(b, h)
            for when, item in waiting:
                if when <= tick:
                    make_operand(item[0], item[1], item[2])
            waiting = [(when, item) for when, item in waiting if when > tick]

        for b, t, bank, c_bank, c_out, width in relus:
            relu(b, t, bank, c_bank, c_out, width)
        for b, a, h, bank in full[0:3:2]:
            leave(b, a, h, bank)
        regroup(LAST, 1024, 1024, ("vector",))
        quantise_hidden(LAST, 1)
        for b, a, h, bank in full[1:4:2]:
            leave(b, a, h, bank)
        free = [hidden_banks[0], flip_banks[0], flip_banks[1], score_banks[0]]
        full = []
        for a in range(4):
            full += scores(LAST, a, (1,), [free[a]])
        for b, a, h, bank in full:
            leave(b, a, h, bank)
